import numpy as np
import ml_dtypes


def mxq(x, axis, fmt="e4m3"):
    dtype, down = {"e4m3": (ml_dtypes.float8_e4m3fn, 7), "e5m2": (ml_dtypes.float8_e5m2, 14)}[fmt]
    v = np.moveaxis(np.asarray(x, np.float32).astype(ml_dtypes.bfloat16).astype(np.float64), axis, -1)
    blocks = v.reshape(v.shape[:-1] + (-1, 32))
    amax = np.abs(blocks).max(-1, keepdims=True)
    byte = np.maximum(np.where(amax > 0, np.frexp(amax)[1] - 1 + 127, 0) - down, 1)
    scale = np.exp2(byte - 127.0)
    codes = (blocks / scale).astype(np.float32).astype(dtype).astype(np.float64)
    return np.moveaxis((codes * scale).reshape(v.shape), -1, axis)


WIDE = False


def mx_kscale(k):
    if not WIDE:
        return np.ones(k)
    levels = np.array([10, -10, 5, -5, 0])
    a = np.random.permutation(np.resize(levels, k // 512 * 4)).reshape(k // 512, 4)
    idx = np.arange(k)
    return np.exp2(a[idx // 512, idx % 128 // 32])


BF16 = ml_dtypes.bfloat16


def bf(x):
    return np.asarray(x, np.float32).astype(BF16)


def f64(x):
    return np.asarray(x).astype(np.float64)


E2M1 = np.array([0.0, 0.5, 1.0, 1.5, 2.0, 3.0, 4.0, 6.0, -0.0, -0.5, -1.0, -1.5, -2.0, -3.0, -4.0, -6.0])


def pack_weight(w, fmt):
    k, n = w.shape
    w = f64(bf(w)).reshape(k // 32, 32, n)
    amax = np.abs(w).max(1)
    if fmt == "e4m3":
        byte = np.frexp(amax)[1] - 1 + 127 - 7
    else:
        mant, ex = np.frexp(amax / 6.0)
        byte = np.where(mant > 0.5, ex, ex - 1) + 127
    byte = np.clip(np.where(amax > 0, byte, 1), 1, 254)
    scaled = (w * np.exp2(127.0 - byte)[:, None, :]).reshape(k, n).astype(np.float32)
    by_word = np.ascontiguousarray(scaled.reshape(k // 512, 128, 4, n).transpose(0, 1, 3, 2))
    if fmt == "e4m3":
        words = by_word.astype(ml_dtypes.float8_e4m3fn).view(np.uint8)
    else:
        c = by_word.astype(ml_dtypes.float4_e2m1fn).view(np.uint8) & 0xF
        words = c[..., 0::2] | (c[..., 1::2] << 4)
    return np.ascontiguousarray(words), np.ascontiguousarray(byte.astype(np.uint8).reshape(k // 512, 16, n))


def unpack_weight(words, scales, fmt):
    g, p, n, _ = words.shape
    if fmt == "e4m3":
        vals = np.ascontiguousarray(words).view(ml_dtypes.float8_e4m3fn).astype(np.float64)
    else:
        nib = np.empty((g, p, n, 4), np.uint8)
        nib[..., 0::2] = words & 0xF
        nib[..., 1::2] = words >> 4
        vals = E2M1[nib]
    vals = vals * np.repeat(np.exp2(scales.astype(np.float64) - 127.0), 8, axis=1)[..., None]
    return vals.transpose(0, 1, 3, 2).reshape(g * 512, n)


B, N, NF, ND, NH = 1, 128, 128, 512, 512


def setup_inputs():
    s = mx_kscale(ND)
    t = mx_kscale(NH)
    atom_features = bf(np.random.standard_normal((B, N, NF)))
    distance_matrix = bf(np.random.random((B, N, N, ND)) * s)
    distance_matrix_mask = bf(0.25 + 0.75 * np.random.random((B, N, N)))
    W_cf = bf(np.random.standard_normal((NF, NH)) / np.sqrt(NF) * t)
    W_df_words, W_df_scales = pack_weight(np.random.standard_normal((ND, NH)) * 1.5 / np.sqrt(ND) / s[:, None], "e4m3")
    W_fc_words, W_fc_scales = pack_weight(np.random.standard_normal((NH, NF)) / np.sqrt(NH) / t[:, None], "e4m3")
    b_cf = bf(np.random.standard_normal(NH) * 0.3 * t)
    b_df = bf(np.random.standard_normal(NH) * 0.3)
    return {
        "atom_features": atom_features,
        "distance_matrix": distance_matrix,
        "distance_matrix_mask": distance_matrix_mask,
        "W_cf": W_cf,
        "W_df_words": W_df_words,
        "W_df_scales": W_df_scales,
        "W_fc_words": W_fc_words,
        "W_fc_scales": W_fc_scales,
        "b_cf": b_cf,
        "b_df": b_df,
    }


def reference(atom_features, distance_matrix, distance_matrix_mask, W_cf, W_df_words, W_df_scales, W_fc_words, W_fc_scales, b_cf, b_df):
    a = f64(atom_features)
    dist_h = (mxq(f64(distance_matrix), 3, "e4m3") @ unpack_weight(W_df_words, W_df_scales, "e4m3")) + f64(b_df)
    atom_h = a @ f64(W_cf) + f64(b_cf)
    gated = dist_h * atom_h[:, None, :, :]
    out = mxq(gated, 3, "e4m3") @ unpack_weight(W_fc_words, W_fc_scales, "e4m3")
    out = out * f64(distance_matrix_mask)[..., None]
    return np.tanh(out).sum(axis=2) + a

@@ -1,0 +1,260 @@
+import concourse.mybir as mybir
+from concourse.masks import make_identity
+
+F32 = mybir.dt.float32
+BF16 = mybir.dt.bfloat16
+I32 = mybir.dt.int32
+U32 = mybir.dt.uint32
+U8 = mybir.dt.uint8
+FP8X4 = mybir.dt.float8_e4m3fn_x4
+ADD = mybir.AluOpType.add
+MULT = mybir.AluOpType.mult
+
+P = 128
+ND = 512
+NH = 512
+CHUNKS = NH // P
+J_ROUND = 4
+ROUNDS = P // J_ROUND
+COLS = J_ROUND * P
+J_BANK = 2
+
+FLOPS = 2 * P * P * ND * NH + 2 * P * P * NH * P + 2 * P * P * NH
+
+LAG_FIRST_MATMUL = 1
+LAG_TO_ROWS = 2
+LAG_TO_WORDS = 3
+LAG_QUANTISE_GATED = 4
+LAG_SECOND_MATMUL = 5
+
+
+def tile_dtnnstep_pa_t_kernel(
+    tc,
+    atom_features,
+    distance_matrix,
+    distance_matrix_mask,
+    W_cf,
+    W_df_words,
+    W_df_scales,
+    W_fc_words,
+    W_fc_scales,
+    b_cf,
+    b_df,
+    out,
+):
+    nc = tc.nc
+    with tc.tile_pool(name="const", bufs=1) as const, tc.tile_pool(name="dist", bufs=1) as dist, tc.tile_pool(
+        name="work", bufs=2
+    ) as work, tc.tile_pool(name="held", bufs=3) as held, tc.psum_pool(name="psum_x", bufs=CHUNKS) as psum_x, tc.psum_pool(
+        name="psum_o", bufs=1
+    ) as psum_o, tc.psum_pool(name="psum_t", bufs=3) as psum_t, tc.manual_schedule():
+        wdf_scales = const.tile([P, NH], U8, align_bytes=64)
+        wfc_scales = const.tile([P, P], U8, align_bytes=64)
+        nc.vector.memset(wdf_scales[:].bitcast(I32), 0)
+        nc.vector.memset(wfc_scales[:].bitcast(I32), 0)
+        bias_rows = const.tile([P, P], BF16)
+        nc.vector.memset(bias_rows[:], 0.0)
+
+        wdf_words = const.tile([P, NH], U32, align_bytes=64)
+        wfc_words = const.tile([P, P], U32, align_bytes=64)
+        nc.sync.dma_start(out=wdf_words[:].bitcast(I32), in_=W_df_words[0].rearrange("p n t -> p (n t)").bitcast(I32))
+        for quad in range(4):
+            nc.sync.dma_start(
+                out=wdf_scales[32 * quad : 32 * quad + 4, :].bitcast(I32),
+                in_=W_df_scales[0, 4 * quad : 4 * quad + 4, :].bitcast(I32),
+            )
+        nc.sync.dma_start(out=wfc_words[:].bitcast(I32), in_=W_fc_words[0].rearrange("p n t -> p (n t)").bitcast(I32))
+        for quad in range(4):
+            nc.sync.dma_start(
+                out=wfc_scales[32 * quad : 32 * quad + 4, :].bitcast(I32),
+                in_=W_fc_scales[0, 4 * quad : 4 * quad + 4, :].bitcast(I32),
+            )
+
+        atoms = const.tile([P, P], BF16)
+        wcf = const.tile([P, NH], BF16)
+        pair_weight_bf = const.tile([P, P], BF16)
+        nc.scalar.dma_start(out=atoms[:], in_=atom_features[0])
+        nc.scalar.dma_start(out=wcf[:], in_=W_cf)
+        nc.scalar.dma_start(out=bias_rows[0:CHUNKS, :], in_=b_cf.rearrange("(c m) -> c m", c=CHUNKS))
+        nc.scalar.dma_start(out=bias_rows[CHUNKS : 2 * CHUNKS, :], in_=b_df.rearrange("(c m) -> c m", c=CHUNKS))
+        nc.scalar.dma_start(out=pair_weight_bf[:], in_=distance_matrix_mask[0])
+
+        dist_rows = {}
+        for r in range(ROUNDS):
+            rows = dist.tile([P, J_ROUND, ND], BF16, name="dist_rows%d" % r)
+            nc.sync.dma_start(out=rows[:], in_=distance_matrix[0, :, J_ROUND * r : J_ROUND * (r + 1), :])
+            dist_rows[r] = rows
+
+        ident_bf = const.tile([P, P], BF16)
+        ident_f32 = const.tile([P, P], F32)
+        make_identity(nc, ident_bf[:])
+        make_identity(nc, ident_f32[:])
+        sort_pairs = const.tile([P, P], BF16)
+        nc.vector.tensor_copy(
+            out=sort_pairs[:].rearrange("m (u q e) -> m u q e", u=2, q=32, e=2),
+            in_=ident_bf[:].rearrange("m (q u e) -> m u q e", q=32, u=2, e=2),
+        )
+
+        pair_weight = const.tile([P, P], F32)
+        nc.vector.tensor_copy(out=pair_weight[:], in_=pair_weight_bf[:])
+
+        bias_ps = psum_t.tile([P, P], BF16, tag="t")
+        nc.tensor.transpose(bias_ps[:], bias_rows[:], ident_bf[:])
+        bias_cols = const.tile([P, 2 * CHUNKS], F32)
+        nc.vector.tensor_copy(out=bias_cols[:], in_=bias_ps[:, 0 : 2 * CHUNKS])
+
+        atoms_t_ps = psum_t.tile([P, P], BF16, tag="t")
+        nc.tensor.transpose(atoms_t_ps[:], atoms[:], ident_bf[:])
+        atoms_t = const.tile([P, P], BF16)
+        nc.vector.tensor_copy(out=atoms_t[:], in_=atoms_t_ps[:])
+
+        atom_h_ps = psum_t.tile([P, CHUNKS, P], F32, tag="t")
+        atom_h_t = const.tile([P, CHUNKS, P], F32)
+        for c in range(CHUNKS):
+            nc.tensor.matmul(atom_h_ps[:, c, :], lhsT=wcf[:, P * c : P * (c + 1)], rhs=atoms_t[:], start=True, stop=True)
+        for c in range(CHUNKS):
+            nc.vector.tensor_scalar_add(out=atom_h_t[:, c, :], in0=atom_h_ps[:, c, :], scalar1=bias_cols[:, c : c + 1])
+
+        total = const.tile([P, J_ROUND, P], F32)
+        nc.vector.memset(total[:], 0.0)
+
+        dist_codes = {}
+        dist_scales = {}
+        gated_h = {}
+        gated_rows = {}
+        gated_word_banks = {}
+        gated_codes = {}
+        gated_scales = {}
+
+        def words_out_of_psum(bank, grouped, half):
+            nc.scalar.copy(
+                out=grouped[:, 4 * P * J_BANK * half : 4 * P * J_BANK * (half + 1)]
+                .bitcast(F32)
+                .rearrange("p (j i u) -> p j i u", j=J_BANK, i=P, u=2),
+                in_=bank[:].rearrange("p j u i -> p j i u"),
+            )
+
+        def transpose_distances(r):
+            words = dist_rows[r][:].bitcast(F32)
+            grouped = work.tile([P, 4 * COLS], BF16, align_bytes=64, name="dist_grouped")
+            for half in range(J_ROUND // J_BANK):
+                bank = psum_t.tile([P, J_BANK, 2, P], F32, tag="t", name="dist_bank")
+                for j in range(J_BANK):
+                    for u in range(2):
+                        nc.tensor.transpose(bank[:, j, u, :], words[:, J_BANK * half + j, u : ND // 2 : 2], ident_f32[:])
+                words_out_of_psum(bank, grouped, half)
+            codes = work.tile([P, COLS], U32, align_bytes=64, name="dist_codes")
+            scales = work.tile([P, COLS], U8, align_bytes=64, name="dist_scales")
+            nc.vector.quantize_mx(out=codes[:].bitcast(FP8X4), scales=scales[:], in_=grouped[:])
+            dist_codes[r] = codes
+            dist_scales[r] = scales
+
+        def first_matmul_and_gate(r):
+            gated = held.tile([P, CHUNKS, COLS], BF16, name="gated_h")
+            for c in range(CHUNKS):
+                acc = psum_x.tile([P, COLS], F32, tag="x", name="dist_h")
+                nc.tensor.matmul_mx(
+                    out=acc[:],
+                    lhsT=wdf_words[:, P * c : P * (c + 1)].bitcast(FP8X4),
+                    lhsT_scale=wdf_scales[:, P * c : P * (c + 1)],
+                    rhs=dist_codes[r][:].bitcast(FP8X4),
+                    rhs_scale=dist_scales[r][:],
+                    start=True,
+                    stop=True,
+                )
+                nc.vector.scalar_tensor_tensor(
+                    out=gated[:, c, :].rearrange("m (j i) -> m j i", j=J_ROUND),
+                    in0=acc[:].rearrange("m (j i) -> m j i", j=J_ROUND),
+                    scalar=bias_cols[:, CHUNKS + c : CHUNKS + c + 1],
+                    in1=atom_h_t[:, c, J_ROUND * r : J_ROUND * (r + 1)].unsqueeze(2).to_broadcast([P, J_ROUND, P]),
+                    op0=ADD,
+                    op1=MULT,
+                )
+            gated_h[r] = gated
+
+        def gated_to_rows(r):
+            rows = held.tile([P, J_ROUND, 2, NH // 2], BF16, name="gated_rows")
+            for half in range(J_ROUND // J_BANK):
+                bank = psum_t.tile([P, J_BANK, 2, NH // 2], BF16, tag="t", name="rows_bank")
+                for j in range(J_BANK):
+                    for c in range(CHUNKS):
+                        first = P * (J_BANK * half + j)
+                        nc.tensor.transpose(
+                            bank[:, j, :, 64 * c : 64 * (c + 1)], gated_h[r][:, c, first : first + P], sort_pairs[:]
+                        )
+                nc.scalar.copy(out=rows[:, J_BANK * half : J_BANK * (half + 1), :, :], in_=bank[:])
+            gated_rows[r] = rows
+
+        def gated_to_words(r):
+            words = gated_rows[r][:].rearrange("i j u w -> i j (u w)").bitcast(F32)
+            banks = []
+            for half in range(J_ROUND // J_BANK):
+                bank = psum_t.tile([P, J_BANK, 2, P], F32, tag="t", name="words_bank")
+                for j in range(J_BANK):
+                    for u in range(2):
+                        nc.tensor.transpose(bank[:, j, u, :], words[:, J_BANK * half + j, P * u : P * (u + 1)], ident_f32[:])
+                banks.append(bank)
+            gated_word_banks[r] = banks
+
+        def group_gated(r):
+            grouped = work.tile([P, 4 * COLS], BF16, align_bytes=64, name="gated_grouped")
+            for half in range(J_ROUND // J_BANK):
+                words_out_of_psum(gated_word_banks[r][half], grouped, half)
+            return grouped
+
+        def quantise_gated(r, grouped):
+            codes = held.tile([P, COLS], U32, align_bytes=64, name="gated_codes")
+            scales = held.tile([P, COLS], U8, align_bytes=64, name="gated_scales")
+            nc.vector.quantize_mx(out=codes[:].bitcast(FP8X4), scales=scales[:], in_=grouped[:])
+            gated_codes[r] = codes
+            gated_scales[r] = scales
+
+        def second_matmul_and_sum(r):
+            acc = psum_o.tile([P, J_ROUND, P], F32, name="pair_out")
+            for j in range(J_ROUND):
+                nc.tensor.matmul_mx(
+                    out=acc[:, j, :],
+                    lhsT=gated_codes[r][:, P * j : P * (j + 1)].bitcast(FP8X4),
+                    lhsT_scale=gated_scales[r][:, P * j : P * (j + 1)],
+                    rhs=wfc_words[:].bitcast(FP8X4),
+                    rhs_scale=wfc_scales[:],
+                    start=True,
+                    stop=True,
+                )
+            squashed = work.tile([P, J_ROUND, P], F32, name="squashed")
+            for j in range(J_ROUND):
+                nc.scalar.activation(
+                    out=squashed[:, j, :],
+                    in_=acc[:, j, :],
+                    func=mybir.ActivationFunctionType.Tanh,
+                    scale=pair_weight[:, J_ROUND * r + j : J_ROUND * r + j + 1],
+                )
+            nc.vector.tensor_tensor(out=total[:], in0=total[:], in1=squashed[:], op=ADD)
+
+        def live(r):
+            return 0 <= r < ROUNDS
+
+        for step in range(ROUNDS + LAG_SECOND_MATMUL):
+            grouped = None
+            if live(step - LAG_QUANTISE_GATED):
+                grouped = group_gated(step - LAG_QUANTISE_GATED)
+            if live(step - LAG_FIRST_MATMUL):
+                first_matmul_and_gate(step - LAG_FIRST_MATMUL)
+            if live(step - LAG_QUANTISE_GATED):
+                quantise_gated(step - LAG_QUANTISE_GATED, grouped)
+            if live(step - LAG_SECOND_MATMUL):
+                second_matmul_and_sum(step - LAG_SECOND_MATMUL)
+            if live(step):
+                transpose_distances(step)
+            if live(step - LAG_TO_ROWS):
+                gated_to_rows(step - LAG_TO_ROWS)
+            if live(step - LAG_TO_WORDS):
+                gated_to_words(step - LAG_TO_WORDS)
+
+        summed = const.tile([P, P], F32)
+        nc.vector.tensor_reduce(
+            out=summed[:], in_=total[:].rearrange("i j n -> i n j"), axis=mybir.AxisListType.X, op=ADD
+        )
+        result = const.tile([P, P], F32)
+        nc.vector.tensor_tensor(out=result[:], in0=summed[:], in1=atoms[:], op=ADD)
+        nc.sync.dma_start(out=out[0], in_=result[:])

@@ -17,15 +17,17 @@ CHUNKS = NH // P
 J_ROUND = 4
 ROUNDS = P // J_ROUND
 COLS = J_ROUND * P
-J_BANK = 2
+J_UNIT = 2
+UNITS = P // J_UNIT
+UNIT_COLS = J_UNIT * P
 
 FLOPS = 2 * P * P * ND * NH + 2 * P * P * NH * P + 2 * P * P * NH
 
-LAG_FIRST_MATMUL = 1
-LAG_TO_ROWS = 2
-LAG_TO_WORDS = 3
-LAG_QUANTISE_GATED = 4
-LAG_SECOND_MATMUL = 5
+LAG_FIRST_MATMUL = 2
+LAG_TO_ROWS = 4
+LAG_TO_WORDS = 5
+LAG_QUANTISE_GATED = 6
+LAG_SECOND_MATMUL = 7
 
 
 def tile_dtnnstep_pa_t_kernel(
@@ -45,9 +47,9 @@ def tile_dtnnstep_pa_t_kernel(
     nc = tc.nc
     with tc.tile_pool(name="const", bufs=1) as const, tc.tile_pool(name="dist", bufs=1) as dist, tc.tile_pool(
         name="work", bufs=2
-    ) as work, tc.tile_pool(name="held", bufs=3) as held, tc.psum_pool(name="psum_x", bufs=CHUNKS) as psum_x, tc.psum_pool(
+    ) as work, tc.tile_pool(name="held", bufs=3) as held, tc.psum_pool(name="psum_x", bufs=3) as psum_x, tc.psum_pool(
         name="psum_o", bufs=1
-    ) as psum_o, tc.psum_pool(name="psum_t", bufs=3) as psum_t, tc.manual_schedule():
+    ) as psum_o, tc.psum_pool(name="psum_t", bufs=4) as psum_t, tc.manual_schedule():
         wdf_scales = const.tile([P, NH], U8, align_bytes=64)
         wfc_scales = const.tile([P, P], U8, align_bytes=64)
         nc.vector.memset(wdf_scales[:].bitcast(I32), 0)
@@ -115,133 +117,121 @@ def tile_dtnnstep_pa_t_kernel(
         for c in range(CHUNKS):
             nc.vector.tensor_scalar_add(out=atom_h_t[:, c, :], in0=atom_h_ps[:, c, :], scalar1=bias_cols[:, c : c + 1])
 
-        total = const.tile([P, J_ROUND, P], F32)
+        total = const.tile([P, J_UNIT, P], F32)
         nc.vector.memset(total[:], 0.0)
 
         dist_codes = {}
         dist_scales = {}
         gated_h = {}
         gated_rows = {}
-        gated_word_banks = {}
+        gated_word_bank = {}
         gated_codes = {}
         gated_scales = {}
 
-        def words_out_of_psum(bank, grouped, half):
+        def words_out_of_psum(bank, grouped):
             nc.scalar.copy(
-                out=grouped[:, 4 * P * J_BANK * half : 4 * P * J_BANK * (half + 1)]
-                .bitcast(F32)
-                .rearrange("p (j i u) -> p j i u", j=J_BANK, i=P, u=2),
+                out=grouped[:].bitcast(F32).rearrange("p (j i u) -> p j i u", j=J_UNIT, i=P, u=2),
                 in_=bank[:].rearrange("p j u i -> p j i u"),
             )
 
-        def transpose_distances(r):
+        def transpose_distances(unit):
+            r, half = divmod(unit, 2)
             words = dist_rows[r][:].bitcast(F32)
-            grouped = work.tile([P, 4 * COLS], BF16, align_bytes=64, name="dist_grouped")
-            for half in range(J_ROUND // J_BANK):
-                bank = psum_t.tile([P, J_BANK, 2, P], F32, tag="t", name="dist_bank")
-                for j in range(J_BANK):
-                    for u in range(2):
-                        nc.tensor.transpose(bank[:, j, u, :], words[:, J_BANK * half + j, u : ND // 2 : 2], ident_f32[:])
-                words_out_of_psum(bank, grouped, half)
-            codes = work.tile([P, COLS], U32, align_bytes=64, name="dist_codes")
-            scales = work.tile([P, COLS], U8, align_bytes=64, name="dist_scales")
-            nc.vector.quantize_mx(out=codes[:].bitcast(FP8X4), scales=scales[:], in_=grouped[:])
-            dist_codes[r] = codes
-            dist_scales[r] = scales
+            bank = psum_t.tile([P, J_UNIT, 2, P], F32, tag="t", name="dist_bank")
+            for j in range(J_UNIT):
+                for u in range(2):
+                    nc.tensor.transpose(bank[:, j, u, :], words[:, J_UNIT * half + j, u : ND // 2 : 2], ident_f32[:])
+            grouped = work.tile([P, 4 * UNIT_COLS], BF16, align_bytes=64, name="dist_grouped")
+            words_out_of_psum(bank, grouped)
+            if half == 0:
+                dist_codes[r] = held.tile([P, COLS], U32, align_bytes=64, name="dist_codes")
+                dist_scales[r] = held.tile([P, COLS], U8, align_bytes=64, name="dist_scales")
+            cols = slice(UNIT_COLS * half, UNIT_COLS * (half + 1))
+            nc.vector.quantize_mx(out=dist_codes[r][:, cols].bitcast(FP8X4), scales=dist_scales[r][:, cols], in_=grouped[:])
 
-        def first_matmul_and_gate(r):
-            gated = held.tile([P, CHUNKS, COLS], BF16, name="gated_h")
-            for c in range(CHUNKS):
-                acc = psum_x.tile([P, COLS], F32, tag="x", name="dist_h")
-                nc.tensor.matmul_mx(
-                    out=acc[:],
-                    lhsT=wdf_words[:, P * c : P * (c + 1)].bitcast(FP8X4),
-                    lhsT_scale=wdf_scales[:, P * c : P * (c + 1)],
-                    rhs=dist_codes[r][:].bitcast(FP8X4),
-                    rhs_scale=dist_scales[r][:],
-                    start=True,
-                    stop=True,
-                )
-                nc.vector.scalar_tensor_tensor(
-                    out=gated[:, c, :].rearrange("m (j i) -> m j i", j=J_ROUND),
-                    in0=acc[:].rearrange("m (j i) -> m j i", j=J_ROUND),
-                    scalar=bias_cols[:, CHUNKS + c : CHUNKS + c + 1],
-                    in1=atom_h_t[:, c, J_ROUND * r : J_ROUND * (r + 1)].unsqueeze(2).to_broadcast([P, J_ROUND, P]),
-                    op0=ADD,
-                    op1=MULT,
-                )
-            gated_h[r] = gated
+        def first_matmul_and_gate(r, c):
+            acc = psum_x.tile([P, COLS], F32, tag="x", name="dist_h")
+            nc.tensor.matmul_mx(
+                out=acc[:],
+                lhsT=wdf_words[:, P * c : P * (c + 1)].bitcast(FP8X4),
+                lhsT_scale=wdf_scales[:, P * c : P * (c + 1)],
+                rhs=dist_codes[r][:].bitcast(FP8X4),
+                rhs_scale=dist_scales[r][:],
+                start=True,
+                stop=True,
+            )
+            nc.vector.scalar_tensor_tensor(
+                out=gated_h[r][:, c, :].rearrange("m (j i) -> m j i", j=J_ROUND),
+                in0=acc[:].rearrange("m (j i) -> m j i", j=J_ROUND),
+                scalar=bias_cols[:, CHUNKS + c : CHUNKS + c + 1],
+                in1=atom_h_t[:, c, J_ROUND * r : J_ROUND * (r + 1)].unsqueeze(2).to_broadcast([P, J_ROUND, P]),
+                op0=ADD,
+                op1=MULT,
+            )
 
-        def gated_to_rows(r):
-            rows = held.tile([P, J_ROUND, 2, NH // 2], BF16, name="gated_rows")
-            for half in range(J_ROUND // J_BANK):
-                bank = psum_t.tile([P, J_BANK, 2, NH // 2], BF16, tag="t", name="rows_bank")
-                for j in range(J_BANK):
-                    for c in range(CHUNKS):
-                        first = P * (J_BANK * half + j)
-                        nc.tensor.transpose(
-                            bank[:, j, :, 64 * c : 64 * (c + 1)], gated_h[r][:, c, first : first + P], sort_pairs[:]
-                        )
-                nc.scalar.copy(out=rows[:, J_BANK * half : J_BANK * (half + 1), :, :], in_=bank[:])
-            gated_rows[r] = rows
+        def gated_to_rows(unit):
+            r, half = divmod(unit, 2)
+            bank = psum_t.tile([P, J_UNIT, 2, NH // 2], BF16, tag="t", name="rows_bank")
+            for j in range(J_UNIT):
+                for c in range(CHUNKS):
+                    first = P * (J_UNIT * half + j)
+                    nc.tensor.transpose(
+                        bank[:, j, :, 64 * c : 64 * (c + 1)], gated_h[r][:, c, first : first + P], sort_pairs[:]
+                    )
+            rows = held.tile([P, J_UNIT, 2, NH // 2], BF16, name="gated_rows")
+            nc.scalar.copy(out=rows[:], in_=bank[:])
+            gated_rows[unit] = rows
 
-        def gated_to_words(r):
-            words = gated_rows[r][:].rearrange("i j u w -> i j (u w)").bitcast(F32)
-            banks = []
-            for half in range(J_ROUND // J_BANK):
-                bank = psum_t.tile([P, J_BANK, 2, P], F32, tag="t", name="words_bank")
-                for j in range(J_BANK):
-                    for u in range(2):
-                        nc.tensor.transpose(bank[:, j, u, :], words[:, J_BANK * half + j, P * u : P * (u + 1)], ident_f32[:])
-                banks.append(bank)
-            gated_word_banks[r] = banks
+        def gated_to_words(unit):
+            words = gated_rows[unit][:].rearrange("i j u w -> i j (u w)").bitcast(F32)
+            bank = psum_t.tile([P, J_UNIT, 2, P], F32, tag="t", name="words_bank")
+            for j in range(J_UNIT):
+                for u in range(2):
+                    nc.tensor.transpose(bank[:, j, u, :], words[:, j, P * u : P * (u + 1)], ident_f32[:])
+            gated_word_bank[unit] = bank
 
-        def group_gated(r):
-            grouped = work.tile([P, 4 * COLS], BF16, align_bytes=64, name="gated_grouped")
-            for half in range(J_ROUND // J_BANK):
-                words_out_of_psum(gated_word_banks[r][half], grouped, half)
-            return grouped
-
-        def quantise_gated(r, grouped):
-            codes = held.tile([P, COLS], U32, align_bytes=64, name="gated_codes")
-            scales = held.tile([P, COLS], U8, align_bytes=64, name="gated_scales")
-            nc.vector.quantize_mx(out=codes[:].bitcast(FP8X4), scales=scales[:], in_=grouped[:])
-            gated_codes[r] = codes
-            gated_scales[r] = scales
-
-        def second_matmul_and_sum(r):
-            acc = psum_o.tile([P, J_ROUND, P], F32, name="pair_out")
-            for j in range(J_ROUND):
+        def second_matmul_and_sum(unit):
+            acc = psum_o.tile([P, J_UNIT, P], F32, name="pair_out")
+            for j in range(J_UNIT):
                 nc.tensor.matmul_mx(
                     out=acc[:, j, :],
-                    lhsT=gated_codes[r][:, P * j : P * (j + 1)].bitcast(FP8X4),
-                    lhsT_scale=gated_scales[r][:, P * j : P * (j + 1)],
+                    lhsT=gated_codes[unit][:, P * j : P * (j + 1)].bitcast(FP8X4),
+                    lhsT_scale=gated_scales[unit][:, P * j : P * (j + 1)],
                     rhs=wfc_words[:].bitcast(FP8X4),
                     rhs_scale=wfc_scales[:],
                     start=True,
                     stop=True,
                 )
-            squashed = work.tile([P, J_ROUND, P], F32, name="squashed")
-            for j in range(J_ROUND):
+            squashed = work.tile([P, J_UNIT, P], F32, name="squashed")
+            for j in range(J_UNIT):
                 nc.scalar.activation(
                     out=squashed[:, j, :],
                     in_=acc[:, j, :],
                     func=mybir.ActivationFunctionType.Tanh,
-                    scale=pair_weight[:, J_ROUND * r + j : J_ROUND * r + j + 1],
+                    scale=pair_weight[:, J_UNIT * unit + j : J_UNIT * unit + j + 1],
                 )
             nc.vector.tensor_tensor(out=total[:], in0=total[:], in1=squashed[:], op=ADD)
 
-        def live(r):
-            return 0 <= r < ROUNDS
+        def live(unit):
+            return 0 <= unit < UNITS
 
-        for step in range(ROUNDS + LAG_SECOND_MATMUL):
-            grouped = None
-            if live(step - LAG_QUANTISE_GATED):
-                grouped = group_gated(step - LAG_QUANTISE_GATED)
+        for step in range(UNITS + LAG_SECOND_MATMUL):
+            quantising = step - LAG_QUANTISE_GATED
+            if live(quantising):
+                grouped = work.tile([P, 4 * UNIT_COLS], BF16, align_bytes=64, name="gated_grouped")
+                words_out_of_psum(gated_word_bank[quantising], grouped)
             if live(step - LAG_FIRST_MATMUL):
-                first_matmul_and_gate(step - LAG_FIRST_MATMUL)
-            if live(step - LAG_QUANTISE_GATED):
-                quantise_gated(step - LAG_QUANTISE_GATED, grouped)
+                r, half = divmod(step - LAG_FIRST_MATMUL, 2)
+                if half == 0:
+                    gated_h[r] = held.tile([P, CHUNKS, COLS], BF16, name="gated_h")
+                first_matmul_and_gate(r, 2 * half)
+                first_matmul_and_gate(r, 2 * half + 1)
+            if live(quantising):
+                gated_codes[quantising] = held.tile([P, UNIT_COLS], U32, align_bytes=64, name="gated_codes")
+                gated_scales[quantising] = held.tile([P, UNIT_COLS], U8, align_bytes=64, name="gated_scales")
+                nc.vector.quantize_mx(
+                    out=gated_codes[quantising][:].bitcast(FP8X4), scales=gated_scales[quantising][:], in_=grouped[:]
+                )
             if live(step - LAG_SECOND_MATMUL):
                 second_matmul_and_sum(step - LAG_SECOND_MATMUL)
             if live(step):

@@ -17,17 +17,15 @@ CHUNKS = NH // P
 J_ROUND = 4
 ROUNDS = P // J_ROUND
 COLS = J_ROUND * P
-J_UNIT = 2
-UNITS = P // J_UNIT
-UNIT_COLS = J_UNIT * P
+J_BANK = 2
 
 FLOPS = 2 * P * P * ND * NH + 2 * P * P * NH * P + 2 * P * P * NH
 
 LAG_FIRST_MATMUL = 2
-LAG_TO_ROWS = 4
-LAG_TO_WORDS = 5
-LAG_QUANTISE_GATED = 6
-LAG_SECOND_MATMUL = 7
+LAG_TO_ROWS = 3
+LAG_TO_WORDS = 4
+LAG_QUANTISE_GATED = 5
+LAG_SECOND_MATMUL = 6
 
 
 def tile_dtnnstep_pa_t_kernel(
@@ -47,9 +45,9 @@ def tile_dtnnstep_pa_t_kernel(
     nc = tc.nc
     with tc.tile_pool(name="const", bufs=1) as const, tc.tile_pool(name="dist", bufs=1) as dist, tc.tile_pool(
         name="work", bufs=2
-    ) as work, tc.tile_pool(name="held", bufs=3) as held, tc.psum_pool(name="psum_x", bufs=3) as psum_x, tc.psum_pool(
-        name="psum_o", bufs=1
-    ) as psum_o, tc.psum_pool(name="psum_t", bufs=4) as psum_t, tc.manual_schedule():
+    ) as work, tc.tile_pool(name="held", bufs=3) as held, tc.psum_pool(name="psum_o", bufs=1) as psum_o, tc.psum_pool(
+        name="psum", bufs=7
+    ) as psum, tc.manual_schedule():
         wdf_scales = const.tile([P, NH], U8, align_bytes=64)
         wfc_scales = const.tile([P, P], U8, align_bytes=64)
         nc.vector.memset(wdf_scales[:].bitcast(I32), 0)
@@ -100,138 +98,150 @@ def tile_dtnnstep_pa_t_kernel(
         pair_weight = const.tile([P, P], F32)
         nc.vector.tensor_copy(out=pair_weight[:], in_=pair_weight_bf[:])
 
-        bias_ps = psum_t.tile([P, P], BF16, tag="t")
+        bias_ps = psum.tile([P, P], BF16, tag="bank")
         nc.tensor.transpose(bias_ps[:], bias_rows[:], ident_bf[:])
         bias_cols = const.tile([P, 2 * CHUNKS], F32)
         nc.vector.tensor_copy(out=bias_cols[:], in_=bias_ps[:, 0 : 2 * CHUNKS])
 
-        atoms_t_ps = psum_t.tile([P, P], BF16, tag="t")
+        atoms_t_ps = psum.tile([P, P], BF16, tag="bank")
         nc.tensor.transpose(atoms_t_ps[:], atoms[:], ident_bf[:])
         atoms_t = const.tile([P, P], BF16)
         nc.vector.tensor_copy(out=atoms_t[:], in_=atoms_t_ps[:])
 
-        atom_h_ps = psum_t.tile([P, CHUNKS, P], F32, tag="t")
+        atom_h_ps = psum.tile([P, CHUNKS, P], F32, tag="bank")
         atom_h_t = const.tile([P, CHUNKS, P], F32)
         for c in range(CHUNKS):
             nc.tensor.matmul(atom_h_ps[:, c, :], lhsT=wcf[:, P * c : P * (c + 1)], rhs=atoms_t[:], start=True, stop=True)
         for c in range(CHUNKS):
             nc.vector.tensor_scalar_add(out=atom_h_t[:, c, :], in0=atom_h_ps[:, c, :], scalar1=bias_cols[:, c : c + 1])
 
-        total = const.tile([P, J_UNIT, P], F32)
+        total = const.tile([P, J_ROUND, P], F32)
         nc.vector.memset(total[:], 0.0)
 
         dist_codes = {}
         dist_scales = {}
         gated_h = {}
         gated_rows = {}
-        gated_word_bank = {}
+        gated_word_banks = {}
         gated_codes = {}
         gated_scales = {}
 
-        def words_out_of_psum(bank, grouped):
+        def words_out_of_psum(bank, grouped, half):
             nc.scalar.copy(
-                out=grouped[:].bitcast(F32).rearrange("p (j i u) -> p j i u", j=J_UNIT, i=P, u=2),
+                out=grouped[:, 4 * P * J_BANK * half : 4 * P * J_BANK * (half + 1)]
+                .bitcast(F32)
+                .rearrange("p (j i u) -> p j i u", j=J_BANK, i=P, u=2),
                 in_=bank[:].rearrange("p j u i -> p j i u"),
             )
 
-        def transpose_distances(unit):
-            r, half = divmod(unit, 2)
+        def transpose_distances(r):
             words = dist_rows[r][:].bitcast(F32)
-            bank = psum_t.tile([P, J_UNIT, 2, P], F32, tag="t", name="dist_bank")
-            for j in range(J_UNIT):
-                for u in range(2):
-                    nc.tensor.transpose(bank[:, j, u, :], words[:, J_UNIT * half + j, u : ND // 2 : 2], ident_f32[:])
-            grouped = work.tile([P, 4 * UNIT_COLS], BF16, align_bytes=64, name="dist_grouped")
-            words_out_of_psum(bank, grouped)
-            if half == 0:
-                dist_codes[r] = held.tile([P, COLS], U32, align_bytes=64, name="dist_codes")
-                dist_scales[r] = held.tile([P, COLS], U8, align_bytes=64, name="dist_scales")
-            cols = slice(UNIT_COLS * half, UNIT_COLS * (half + 1))
-            nc.vector.quantize_mx(out=dist_codes[r][:, cols].bitcast(FP8X4), scales=dist_scales[r][:, cols], in_=grouped[:])
+            grouped = work.tile([P, 4 * COLS], BF16, align_bytes=64, name="dist_grouped")
+            for half in range(J_ROUND // J_BANK):
+                bank = psum.tile([P, J_BANK, 2, P], F32, tag="bank", name="dist_bank")
+                for j in range(J_BANK):
+                    for u in range(2):
+                        nc.tensor.transpose(bank[:, j, u, :], words[:, J_BANK * half + j, u : ND // 2 : 2], ident_f32[:])
+                words_out_of_psum(bank, grouped, half)
+            codes = held.tile([P, COLS], U32, align_bytes=64, name="dist_codes")
+            scales = held.tile([P, COLS], U8, align_bytes=64, name="dist_scales")
+            nc.vector.quantize_mx(out=codes[:].bitcast(FP8X4), scales=scales[:], in_=grouped[:])
+            dist_codes[r] = codes
+            dist_scales[r] = scales
 
-        def first_matmul_and_gate(r, c):
-            acc = psum_x.tile([P, COLS], F32, tag="x", name="dist_h")
-            nc.tensor.matmul_mx(
-                out=acc[:],
-                lhsT=wdf_words[:, P * c : P * (c + 1)].bitcast(FP8X4),
-                lhsT_scale=wdf_scales[:, P * c : P * (c + 1)],
-                rhs=dist_codes[r][:].bitcast(FP8X4),
-                rhs_scale=dist_scales[r][:],
-                start=True,
-                stop=True,
-            )
-            nc.vector.scalar_tensor_tensor(
-                out=gated_h[r][:, c, :].rearrange("m (j i) -> m j i", j=J_ROUND),
-                in0=acc[:].rearrange("m (j i) -> m j i", j=J_ROUND),
-                scalar=bias_cols[:, CHUNKS + c : CHUNKS + c + 1],
-                in1=atom_h_t[:, c, J_ROUND * r : J_ROUND * (r + 1)].unsqueeze(2).to_broadcast([P, J_ROUND, P]),
-                op0=ADD,
-                op1=MULT,
-            )
+        def first_matmul_and_gate(r):
+            gated = held.tile([P, CHUNKS, COLS], BF16, name="gated_h")
+            for c in range(CHUNKS):
+                acc = psum.tile([P, COLS], F32, tag="bank", name="dist_h")
+                nc.tensor.matmul_mx(
+                    out=acc[:],
+                    lhsT=wdf_words[:, P * c : P * (c + 1)].bitcast(FP8X4),
+                    lhsT_scale=wdf_scales[:, P * c : P * (c + 1)],
+                    rhs=dist_codes[r][:].bitcast(FP8X4),
+                    rhs_scale=dist_scales[r][:],
+                    start=True,
+                    stop=True,
+                )
+                nc.vector.scalar_tensor_tensor(
+                    out=gated[:, c, :].rearrange("m (j i) -> m j i", j=J_ROUND),
+                    in0=acc[:].rearrange("m (j i) -> m j i", j=J_ROUND),
+                    scalar=bias_cols[:, CHUNKS + c : CHUNKS + c + 1],
+                    in1=atom_h_t[:, c, J_ROUND * r : J_ROUND * (r + 1)].unsqueeze(2).to_broadcast([P, J_ROUND, P]),
+                    op0=ADD,
+                    op1=MULT,
+                )
+            gated_h[r] = gated
 
-        def gated_to_rows(unit):
-            r, half = divmod(unit, 2)
-            bank = psum_t.tile([P, J_UNIT, 2, NH // 2], BF16, tag="t", name="rows_bank")
-            for j in range(J_UNIT):
-                for c in range(CHUNKS):
-                    first = P * (J_UNIT * half + j)
-                    nc.tensor.transpose(
-                        bank[:, j, :, 64 * c : 64 * (c + 1)], gated_h[r][:, c, first : first + P], sort_pairs[:]
-                    )
-            rows = held.tile([P, J_UNIT, 2, NH // 2], BF16, name="gated_rows")
-            nc.scalar.copy(out=rows[:], in_=bank[:])
-            gated_rows[unit] = rows
+        def gated_to_rows(r):
+            rows = held.tile([P, J_ROUND, 2, NH // 2], BF16, name="gated_rows")
+            for half in range(J_ROUND // J_BANK):
+                bank = psum.tile([P, J_BANK, 2, NH // 2], BF16, tag="bank", name="rows_bank")
+                for j in range(J_BANK):
+                    for c in range(CHUNKS):
+                        first = P * (J_BANK * half + j)
+                        nc.tensor.transpose(
+                            bank[:, j, :, 64 * c : 64 * (c + 1)], gated_h[r][:, c, first : first + P], sort_pairs[:]
+                        )
+                nc.scalar.copy(out=rows[:, J_BANK * half : J_BANK * (half + 1), :, :], in_=bank[:])
+            gated_rows[r] = rows
 
-        def gated_to_words(unit):
-            words = gated_rows[unit][:].rearrange("i j u w -> i j (u w)").bitcast(F32)
-            bank = psum_t.tile([P, J_UNIT, 2, P], F32, tag="t", name="words_bank")
-            for j in range(J_UNIT):
-                for u in range(2):
-                    nc.tensor.transpose(bank[:, j, u, :], words[:, j, P * u : P * (u + 1)], ident_f32[:])
-            gated_word_bank[unit] = bank
+        def gated_to_words(r):
+            words = gated_rows[r][:].rearrange("i j u w -> i j (u w)").bitcast(F32)
+            banks = []
+            for half in range(J_ROUND // J_BANK):
+                bank = psum.tile([P, J_BANK, 2, P], F32, tag="bank", name="words_bank")
+                for j in range(J_BANK):
+                    for u in range(2):
+                        nc.tensor.transpose(bank[:, j, u, :], words[:, J_BANK * half + j, P * u : P * (u + 1)], ident_f32[:])
+                banks.append(bank)
+            gated_word_banks[r] = banks
 
-        def second_matmul_and_sum(unit):
-            acc = psum_o.tile([P, J_UNIT, P], F32, name="pair_out")
-            for j in range(J_UNIT):
+        def group_gated(r):
+            grouped = work.tile([P, 4 * COLS], BF16, align_bytes=64, name="gated_grouped")
+            for half in range(J_ROUND // J_BANK):
+                words_out_of_psum(gated_word_banks[r][half], grouped, half)
+            return grouped
+
+        def quantise_gated(r, grouped):
+            codes = held.tile([P, COLS], U32, align_bytes=64, name="gated_codes")
+            scales = held.tile([P, COLS], U8, align_bytes=64, name="gated_scales")
+            nc.vector.quantize_mx(out=codes[:].bitcast(FP8X4), scales=scales[:], in_=grouped[:])
+            gated_codes[r] = codes
+            gated_scales[r] = scales
+
+        def second_matmul_and_sum(r):
+            acc = psum_o.tile([P, J_ROUND, P], F32, name="pair_out")
+            for j in range(J_ROUND):
                 nc.tensor.matmul_mx(
                     out=acc[:, j, :],
-                    lhsT=gated_codes[unit][:, P * j : P * (j + 1)].bitcast(FP8X4),
-                    lhsT_scale=gated_scales[unit][:, P * j : P * (j + 1)],
+                    lhsT=gated_codes[r][:, P * j : P * (j + 1)].bitcast(FP8X4),
+                    lhsT_scale=gated_scales[r][:, P * j : P * (j + 1)],
                     rhs=wfc_words[:].bitcast(FP8X4),
                     rhs_scale=wfc_scales[:],
                     start=True,
                     stop=True,
                 )
-            squashed = work.tile([P, J_UNIT, P], F32, name="squashed")
-            for j in range(J_UNIT):
+            squashed = work.tile([P, J_ROUND, P], F32, name="squashed")
+            for j in range(J_ROUND):
                 nc.scalar.activation(
                     out=squashed[:, j, :],
                     in_=acc[:, j, :],
                     func=mybir.ActivationFunctionType.Tanh,
-                    scale=pair_weight[:, J_UNIT * unit + j : J_UNIT * unit + j + 1],
+                    scale=pair_weight[:, J_ROUND * r + j : J_ROUND * r + j + 1],
                 )
             nc.vector.tensor_tensor(out=total[:], in0=total[:], in1=squashed[:], op=ADD)
 
-        def live(unit):
-            return 0 <= unit < UNITS
+        def live(r):
+            return 0 <= r < ROUNDS
 
-        for step in range(UNITS + LAG_SECOND_MATMUL):
-            quantising = step - LAG_QUANTISE_GATED
-            if live(quantising):
-                grouped = work.tile([P, 4 * UNIT_COLS], BF16, align_bytes=64, name="gated_grouped")
-                words_out_of_psum(gated_word_bank[quantising], grouped)
+        for step in range(ROUNDS + LAG_SECOND_MATMUL):
+            grouped = None
+            if live(step - LAG_QUANTISE_GATED):
+                grouped = group_gated(step - LAG_QUANTISE_GATED)
             if live(step - LAG_FIRST_MATMUL):
-                r, half = divmod(step - LAG_FIRST_MATMUL, 2)
-                if half == 0:
-                    gated_h[r] = held.tile([P, CHUNKS, COLS], BF16, name="gated_h")
-                first_matmul_and_gate(r, 2 * half)
-                first_matmul_and_gate(r, 2 * half + 1)
-            if live(quantising):
-                gated_codes[quantising] = held.tile([P, UNIT_COLS], U32, align_bytes=64, name="gated_codes")
-                gated_scales[quantising] = held.tile([P, UNIT_COLS], U8, align_bytes=64, name="gated_scales")
-                nc.vector.quantize_mx(
-                    out=gated_codes[quantising][:].bitcast(FP8X4), scales=gated_scales[quantising][:], in_=grouped[:]
-                )
+                first_matmul_and_gate(step - LAG_FIRST_MATMUL)
+            if live(step - LAG_QUANTISE_GATED):
+                quantise_gated(step - LAG_QUANTISE_GATED, grouped)
             if live(step - LAG_SECOND_MATMUL):
                 second_matmul_and_sum(step - LAG_SECOND_MATMUL)
             if live(step):

@@ -13,11 +13,20 @@ MULT = mybir.AluOpType.mult
 P = 128
 ND = 512
 NH = 512
+WORD = 4
+PAIRS = 2
+PAIR = 2
 CHUNKS = NH // P
+CHUNK_WORDS = P // WORD
+QUADRANTS = 4
+QUADRANT = P // QUADRANTS
+SCALE_ROWS = 4
+
 J_ROUND = 4
 ROUNDS = P // J_ROUND
 COLS = J_ROUND * P
 J_BANK = 2
+BANKS_ROUND = J_ROUND // J_BANK
 
 FLOPS = 2 * P * P * ND * NH + 2 * P * P * NH * P + 2 * P * P * NH
 
@@ -48,6 +57,16 @@ def tile_dtnnstep_pa_t_kernel(
     ) as work, tc.tile_pool(name="held", bufs=3) as held, tc.psum_pool(name="psum_o", bufs=1) as psum_o, tc.psum_pool(
         name="psum", bufs=7
     ) as psum, tc.manual_schedule():
+        dist_rows = {}
+
+        def load_distance_rows(r):
+            rows = dist.tile([P, J_ROUND, ND], BF16, name="dist_rows%d" % r)
+            nc.sync.dma_start(out=rows[:], in_=distance_matrix[0, :, J_ROUND * r : J_ROUND * (r + 1), :])
+            dist_rows[r] = rows
+
+        for r in range(LAG_FIRST_MATMUL):
+            load_distance_rows(r)
+
         wdf_scales = const.tile([P, NH], U8, align_bytes=64)
         wfc_scales = const.tile([P, P], U8, align_bytes=64)
         nc.vector.memset(wdf_scales[:].bitcast(I32), 0)
@@ -58,16 +77,16 @@ def tile_dtnnstep_pa_t_kernel(
         wdf_words = const.tile([P, NH], U32, align_bytes=64)
         wfc_words = const.tile([P, P], U32, align_bytes=64)
         nc.sync.dma_start(out=wdf_words[:].bitcast(I32), in_=W_df_words[0].rearrange("p n t -> p (n t)").bitcast(I32))
-        for quad in range(4):
+        for quad in range(QUADRANTS):
             nc.sync.dma_start(
-                out=wdf_scales[32 * quad : 32 * quad + 4, :].bitcast(I32),
-                in_=W_df_scales[0, 4 * quad : 4 * quad + 4, :].bitcast(I32),
+                out=wdf_scales[QUADRANT * quad : QUADRANT * quad + SCALE_ROWS, :].bitcast(I32),
+                in_=W_df_scales[0, SCALE_ROWS * quad : SCALE_ROWS * (quad + 1), :].bitcast(I32),
             )
         nc.sync.dma_start(out=wfc_words[:].bitcast(I32), in_=W_fc_words[0].rearrange("p n t -> p (n t)").bitcast(I32))
-        for quad in range(4):
+        for quad in range(QUADRANTS):
             nc.sync.dma_start(
-                out=wfc_scales[32 * quad : 32 * quad + 4, :].bitcast(I32),
-                in_=W_fc_scales[0, 4 * quad : 4 * quad + 4, :].bitcast(I32),
+                out=wfc_scales[QUADRANT * quad : QUADRANT * quad + SCALE_ROWS, :].bitcast(I32),
+                in_=W_fc_scales[0, SCALE_ROWS * quad : SCALE_ROWS * (quad + 1), :].bitcast(I32),
             )
 
         atoms = const.tile([P, P], BF16)
@@ -79,20 +98,17 @@ def tile_dtnnstep_pa_t_kernel(
         nc.scalar.dma_start(out=bias_rows[CHUNKS : 2 * CHUNKS, :], in_=b_df.rearrange("(c m) -> c m", c=CHUNKS))
         nc.scalar.dma_start(out=pair_weight_bf[:], in_=distance_matrix_mask[0])
 
-        dist_rows = {}
-        for r in range(ROUNDS):
-            rows = dist.tile([P, J_ROUND, ND], BF16, name="dist_rows%d" % r)
-            nc.sync.dma_start(out=rows[:], in_=distance_matrix[0, :, J_ROUND * r : J_ROUND * (r + 1), :])
-            dist_rows[r] = rows
+        for r in range(LAG_FIRST_MATMUL, ROUNDS):
+            load_distance_rows(r)
 
         ident_bf = const.tile([P, P], BF16)
         ident_f32 = const.tile([P, P], F32)
-        make_identity(nc, ident_bf[:])
         make_identity(nc, ident_f32[:])
+        make_identity(nc, ident_bf[:])
         sort_pairs = const.tile([P, P], BF16)
         nc.vector.tensor_copy(
-            out=sort_pairs[:].rearrange("m (u q e) -> m u q e", u=2, q=32, e=2),
-            in_=ident_bf[:].rearrange("m (q u e) -> m u q e", q=32, u=2, e=2),
+            out=sort_pairs[:].rearrange("m (u w e) -> m u w e", u=PAIRS, w=CHUNK_WORDS, e=PAIR),
+            in_=ident_bf[:].rearrange("m (w u e) -> m u w e", w=CHUNK_WORDS, u=PAIRS, e=PAIR),
         )
 
         pair_weight = const.tile([P, P], F32)
@@ -122,27 +138,28 @@ def tile_dtnnstep_pa_t_kernel(
         dist_scales = {}
         gated_h = {}
         gated_rows = {}
-        gated_word_banks = {}
+        gated_pair_banks = {}
+        gated_grouped = {}
         gated_codes = {}
         gated_scales = {}
 
-        def words_out_of_psum(bank, grouped, half):
+        def pairs_out_of_psum(bank, grouped, b):
             nc.scalar.copy(
-                out=grouped[:, 4 * P * J_BANK * half : 4 * P * J_BANK * (half + 1)]
+                out=grouped[:, WORD * P * J_BANK * b : WORD * P * J_BANK * (b + 1)]
                 .bitcast(F32)
-                .rearrange("p (j i u) -> p j i u", j=J_BANK, i=P, u=2),
+                .rearrange("p (j i u) -> p j i u", j=J_BANK, i=P, u=PAIRS),
                 in_=bank[:].rearrange("p j u i -> p j i u"),
             )
 
-        def transpose_distances(r):
-            words = dist_rows[r][:].bitcast(F32)
-            grouped = work.tile([P, 4 * COLS], BF16, align_bytes=64, name="dist_grouped")
-            for half in range(J_ROUND // J_BANK):
-                bank = psum.tile([P, J_BANK, 2, P], F32, tag="bank", name="dist_bank")
+        def transpose_and_quantise_distances(r):
+            pairs = dist_rows[r][:].bitcast(F32)
+            grouped = work.tile([P, WORD * COLS], BF16, align_bytes=64, name="dist_grouped")
+            for b in range(BANKS_ROUND):
+                bank = psum.tile([P, J_BANK, PAIRS, P], F32, tag="bank", name="dist_bank")
                 for j in range(J_BANK):
-                    for u in range(2):
-                        nc.tensor.transpose(bank[:, j, u, :], words[:, J_BANK * half + j, u : ND // 2 : 2], ident_f32[:])
-                words_out_of_psum(bank, grouped, half)
+                    for u in range(PAIRS):
+                        nc.tensor.transpose(bank[:, j, u, :], pairs[:, J_BANK * b + j, u : ND // PAIR : PAIRS], ident_f32[:])
+                pairs_out_of_psum(bank, grouped, b)
             codes = held.tile([P, COLS], U32, align_bytes=64, name="dist_codes")
             scales = held.tile([P, COLS], U8, align_bytes=64, name="dist_scales")
             nc.vector.quantize_mx(out=codes[:].bitcast(FP8X4), scales=scales[:], in_=grouped[:])
@@ -173,61 +190,64 @@ def tile_dtnnstep_pa_t_kernel(
             gated_h[r] = gated
 
         def gated_to_rows(r):
-            rows = held.tile([P, J_ROUND, 2, NH // 2], BF16, name="gated_rows")
-            for half in range(J_ROUND // J_BANK):
-                bank = psum.tile([P, J_BANK, 2, NH // 2], BF16, tag="bank", name="rows_bank")
+            rows = held.tile([P, J_ROUND, PAIRS, NH // PAIRS], BF16, name="gated_rows")
+            chunk_cols = CHUNK_WORDS * PAIR
+            for b in range(BANKS_ROUND):
+                bank = psum.tile([P, J_BANK, PAIRS, NH // PAIRS], BF16, tag="bank", name="rows_bank")
                 for j in range(J_BANK):
                     for c in range(CHUNKS):
-                        first = P * (J_BANK * half + j)
+                        first = P * (J_BANK * b + j)
                         nc.tensor.transpose(
-                            bank[:, j, :, 64 * c : 64 * (c + 1)], gated_h[r][:, c, first : first + P], sort_pairs[:]
+                            bank[:, j, :, chunk_cols * c : chunk_cols * (c + 1)],
+                            gated_h[r][:, c, first : first + P],
+                            sort_pairs[:],
                         )
-                nc.scalar.copy(out=rows[:, J_BANK * half : J_BANK * (half + 1), :, :], in_=bank[:])
+                nc.scalar.copy(out=rows[:, J_BANK * b : J_BANK * (b + 1), :, :], in_=bank[:])
             gated_rows[r] = rows
 
-        def gated_to_words(r):
-            words = gated_rows[r][:].rearrange("i j u w -> i j (u w)").bitcast(F32)
+        def gated_to_pairs(r):
+            pairs = gated_rows[r][:].rearrange("i j u w -> i j (u w)").bitcast(F32)
             banks = []
-            for half in range(J_ROUND // J_BANK):
-                bank = psum.tile([P, J_BANK, 2, P], F32, tag="bank", name="words_bank")
+            for b in range(BANKS_ROUND):
+                bank = psum.tile([P, J_BANK, PAIRS, P], F32, tag="bank", name="words_bank")
                 for j in range(J_BANK):
-                    for u in range(2):
-                        nc.tensor.transpose(bank[:, j, u, :], words[:, J_BANK * half + j, P * u : P * (u + 1)], ident_f32[:])
+                    for u in range(PAIRS):
+                        nc.tensor.transpose(bank[:, j, u, :], pairs[:, J_BANK * b + j, P * u : P * (u + 1)], ident_f32[:])
                 banks.append(bank)
-            gated_word_banks[r] = banks
+            gated_pair_banks[r] = banks
 
         def group_gated(r):
-            grouped = work.tile([P, 4 * COLS], BF16, align_bytes=64, name="gated_grouped")
-            for half in range(J_ROUND // J_BANK):
-                words_out_of_psum(gated_word_banks[r][half], grouped, half)
-            return grouped
+            grouped = work.tile([P, WORD * COLS], BF16, align_bytes=64, name="gated_grouped")
+            for b in range(BANKS_ROUND):
+                pairs_out_of_psum(gated_pair_banks[r][b], grouped, b)
+            gated_grouped[r] = grouped
 
-        def quantise_gated(r, grouped):
+        def quantise_gated(r):
             codes = held.tile([P, COLS], U32, align_bytes=64, name="gated_codes")
             scales = held.tile([P, COLS], U8, align_bytes=64, name="gated_scales")
-            nc.vector.quantize_mx(out=codes[:].bitcast(FP8X4), scales=scales[:], in_=grouped[:])
+            nc.vector.quantize_mx(out=codes[:].bitcast(FP8X4), scales=scales[:], in_=gated_grouped[r][:])
             gated_codes[r] = codes
             gated_scales[r] = scales
 
         def second_matmul_and_sum(r):
             acc = psum_o.tile([P, J_ROUND, P], F32, name="pair_out")
-            for j in range(J_ROUND):
+            for s in range(J_ROUND):
                 nc.tensor.matmul_mx(
-                    out=acc[:, j, :],
-                    lhsT=gated_codes[r][:, P * j : P * (j + 1)].bitcast(FP8X4),
-                    lhsT_scale=gated_scales[r][:, P * j : P * (j + 1)],
+                    out=acc[:, s, :],
+                    lhsT=gated_codes[r][:, P * s : P * (s + 1)].bitcast(FP8X4),
+                    lhsT_scale=gated_scales[r][:, P * s : P * (s + 1)],
                     rhs=wfc_words[:].bitcast(FP8X4),
                     rhs_scale=wfc_scales[:],
                     start=True,
                     stop=True,
                 )
             squashed = work.tile([P, J_ROUND, P], F32, name="squashed")
-            for j in range(J_ROUND):
+            for s in range(J_ROUND):
                 nc.scalar.activation(
-                    out=squashed[:, j, :],
-                    in_=acc[:, j, :],
+                    out=squashed[:, s, :],
+                    in_=acc[:, s, :],
                     func=mybir.ActivationFunctionType.Tanh,
-                    scale=pair_weight[:, J_ROUND * r + j : J_ROUND * r + j + 1],
+                    scale=pair_weight[:, J_ROUND * r + s : J_ROUND * r + s + 1],
                 )
             nc.vector.tensor_tensor(out=total[:], in0=total[:], in1=squashed[:], op=ADD)
 
@@ -235,25 +255,24 @@ def tile_dtnnstep_pa_t_kernel(
             return 0 <= r < ROUNDS
 
         for step in range(ROUNDS + LAG_SECOND_MATMUL):
-            grouped = None
             if live(step - LAG_QUANTISE_GATED):
-                grouped = group_gated(step - LAG_QUANTISE_GATED)
+                group_gated(step - LAG_QUANTISE_GATED)
             if live(step - LAG_FIRST_MATMUL):
                 first_matmul_and_gate(step - LAG_FIRST_MATMUL)
             if live(step - LAG_QUANTISE_GATED):
-                quantise_gated(step - LAG_QUANTISE_GATED, grouped)
+                quantise_gated(step - LAG_QUANTISE_GATED)
             if live(step - LAG_SECOND_MATMUL):
                 second_matmul_and_sum(step - LAG_SECOND_MATMUL)
             if live(step):
-                transpose_distances(step)
+                transpose_and_quantise_distances(step)
             if live(step - LAG_TO_ROWS):
                 gated_to_rows(step - LAG_TO_ROWS)
             if live(step - LAG_TO_WORDS):
-                gated_to_words(step - LAG_TO_WORDS)
+                gated_to_pairs(step - LAG_TO_WORDS)
 
         summed = const.tile([P, P], F32)
         nc.vector.tensor_reduce(
-            out=summed[:], in_=total[:].rearrange("i j n -> i n j"), axis=mybir.AxisListType.X, op=ADD
+            out=summed[:], in_=total[:].rearrange("i s n -> i n s"), axis=mybir.AxisListType.X, op=ADD
         )
         result = const.tile([P, P], F32)
         nc.vector.tensor_tensor(out=result[:], in0=summed[:], in1=atoms[:], op=ADD)

@@ -9,6 +9,7 @@ U8 = mybir.dt.uint8
 FP8X4 = mybir.dt.float8_e4m3fn_x4
 ADD = mybir.AluOpType.add
 MULT = mybir.AluOpType.mult
+ACT = mybir.ActivationFunctionType
 
 P = 128
 ND = 512
@@ -16,8 +17,6 @@ NH = 512
 WORD = 4
 PAIRS = 2
 PAIR = 2
-CHUNKS = NH // P
-CHUNK_WORDS = P // WORD
 QUADRANTS = 4
 QUADRANT = P // QUADRANTS
 SCALE_ROWS = 4
@@ -28,13 +27,15 @@ COLS = J_ROUND * P
 J_BANK = 2
 BANKS_ROUND = J_ROUND // J_BANK
 
+SLOTS_SCALAR = 3
+
 FLOPS = 2 * P * P * ND * NH + 2 * P * P * NH * P + 2 * P * P * NH
 
+LAG_QUANTISE_DISTANCES = 1
 LAG_FIRST_MATMUL = 2
-LAG_TO_ROWS = 3
-LAG_TO_WORDS = 4
-LAG_QUANTISE_GATED = 5
-LAG_SECOND_MATMUL = 6
+LAG_QUANTISE_GATED = 3
+LAG_SECOND_MATMUL = 4
+LAG_SUM = 5
 
 
 def tile_dtnnstep_pa_t_kernel(
@@ -67,19 +68,19 @@ def tile_dtnnstep_pa_t_kernel(
         for r in range(LAG_FIRST_MATMUL):
             load_distance_rows(r)
 
-        wdf_scales = const.tile([P, NH], U8, align_bytes=64)
+        wdf_scales_loaded = const.tile([P, NH], U8, align_bytes=64)
         wfc_scales = const.tile([P, P], U8, align_bytes=64)
-        nc.vector.memset(wdf_scales[:].bitcast(I32), 0)
+        nc.vector.memset(wdf_scales_loaded[:].bitcast(I32), 0)
         nc.vector.memset(wfc_scales[:].bitcast(I32), 0)
-        bias_rows = const.tile([P, P], BF16)
-        nc.vector.memset(bias_rows[:], 0.0)
 
-        wdf_words = const.tile([P, NH], U32, align_bytes=64)
+        wdf_words_loaded = const.tile([P, NH], U32, align_bytes=64)
         wfc_words = const.tile([P, P], U32, align_bytes=64)
-        nc.sync.dma_start(out=wdf_words[:].bitcast(I32), in_=W_df_words[0].rearrange("p n t -> p (n t)").bitcast(I32))
+        nc.sync.dma_start(
+            out=wdf_words_loaded[:].bitcast(I32), in_=W_df_words[0].rearrange("p n t -> p (n t)").bitcast(I32)
+        )
         for quad in range(QUADRANTS):
             nc.sync.dma_start(
-                out=wdf_scales[QUADRANT * quad : QUADRANT * quad + SCALE_ROWS, :].bitcast(I32),
+                out=wdf_scales_loaded[QUADRANT * quad : QUADRANT * quad + SCALE_ROWS, :].bitcast(I32),
                 in_=W_df_scales[0, SCALE_ROWS * quad : SCALE_ROWS * (quad + 1), :].bitcast(I32),
             )
         nc.sync.dma_start(out=wfc_words[:].bitcast(I32), in_=W_fc_words[0].rearrange("p n t -> p (n t)").bitcast(I32))
@@ -90,13 +91,20 @@ def tile_dtnnstep_pa_t_kernel(
             )
 
         atoms = const.tile([P, P], BF16)
-        wcf = const.tile([P, NH], BF16)
+        wcf_loaded = const.tile([P, NH], BF16)
         pair_weight_bf = const.tile([P, P], BF16)
+        bcf_bf = const.tile([P, WORD], BF16)
+        bdf_bf = const.tile([P, WORD], BF16)
         nc.scalar.dma_start(out=atoms[:], in_=atom_features[0])
-        nc.scalar.dma_start(out=wcf[:], in_=W_cf)
-        nc.scalar.dma_start(out=bias_rows[0:CHUNKS, :], in_=b_cf.rearrange("(c m) -> c m", c=CHUNKS))
-        nc.scalar.dma_start(out=bias_rows[CHUNKS : 2 * CHUNKS, :], in_=b_df.rearrange("(c m) -> c m", c=CHUNKS))
+        nc.scalar.dma_start(out=wcf_loaded[:], in_=W_cf)
+        nc.scalar.dma_start(out=bcf_bf[:], in_=b_cf.rearrange("(p t) -> p t", t=WORD))
+        nc.scalar.dma_start(out=bdf_bf[:], in_=b_df.rearrange("(p t) -> p t", t=WORD))
         nc.scalar.dma_start(out=pair_weight_bf[:], in_=distance_matrix_mask[0])
+
+        warm_in = const.tile([P, 1], F32)
+        warm_out = const.tile([P, 1], F32)
+        nc.vector.memset(warm_in[:], 0.0)
+        nc.scalar.activation(out=warm_out[:], in_=warm_in[:], func=ACT.Tanh)
 
         for r in range(LAG_FIRST_MATMUL, ROUNDS):
             load_distance_rows(r)
@@ -105,131 +113,138 @@ def tile_dtnnstep_pa_t_kernel(
         ident_f32 = const.tile([P, P], F32)
         make_identity(nc, ident_f32[:])
         make_identity(nc, ident_bf[:])
-        sort_pairs = const.tile([P, P], BF16)
+
+        wdf_words = const.tile([P, NH], U32, align_bytes=64)
+        wdf_scales = const.tile([P, NH], U8, align_bytes=64)
         nc.vector.tensor_copy(
-            out=sort_pairs[:].rearrange("m (u w e) -> m u w e", u=PAIRS, w=CHUNK_WORDS, e=PAIR),
-            in_=ident_bf[:].rearrange("m (w u e) -> m u w e", w=CHUNK_WORDS, u=PAIRS, e=PAIR),
+            out=wdf_words[:].bitcast(I32).rearrange("p (t m) -> p t m", t=WORD),
+            in_=wdf_words_loaded[:].bitcast(I32).rearrange("p (m t) -> p t m", t=WORD),
         )
+        nc.vector.tensor_copy(
+            out=wdf_scales[:].rearrange("p (t m) -> p m t", t=WORD),
+            in_=wdf_scales_loaded[:].rearrange("p (m t) -> p m t", t=WORD),
+        )
+        wcf = const.tile([P, WORD, P], BF16)
+        nc.vector.tensor_copy(out=wcf[:], in_=wcf_loaded[:].rearrange("f (m t) -> f t m", t=WORD))
 
         pair_weight = const.tile([P, P], F32)
         nc.vector.tensor_copy(out=pair_weight[:], in_=pair_weight_bf[:])
-
-        bias_ps = psum.tile([P, P], BF16, tag="bank")
-        nc.tensor.transpose(bias_ps[:], bias_rows[:], ident_bf[:])
-        bias_cols = const.tile([P, 2 * CHUNKS], F32)
-        nc.vector.tensor_copy(out=bias_cols[:], in_=bias_ps[:, 0 : 2 * CHUNKS])
+        bcf = const.tile([P, WORD], F32)
+        bdf = const.tile([P, WORD], F32)
+        nc.vector.tensor_copy(out=bcf[:], in_=bcf_bf[:])
+        nc.vector.tensor_copy(out=bdf[:], in_=bdf_bf[:])
 
         atoms_t_ps = psum.tile([P, P], BF16, tag="bank")
         nc.tensor.transpose(atoms_t_ps[:], atoms[:], ident_bf[:])
         atoms_t = const.tile([P, P], BF16)
         nc.vector.tensor_copy(out=atoms_t[:], in_=atoms_t_ps[:])
 
-        atom_h_ps = psum.tile([P, CHUNKS, P], F32, tag="bank")
-        atom_h_t = const.tile([P, CHUNKS, P], F32)
-        for c in range(CHUNKS):
-            nc.tensor.matmul(atom_h_ps[:, c, :], lhsT=wcf[:, P * c : P * (c + 1)], rhs=atoms_t[:], start=True, stop=True)
-        for c in range(CHUNKS):
-            nc.vector.tensor_scalar_add(out=atom_h_t[:, c, :], in0=atom_h_ps[:, c, :], scalar1=bias_cols[:, c : c + 1])
+        atom_h_ps = psum.tile([P, WORD, P], F32, tag="bank")
+        gate = const.tile([P, WORD, P], F32)
+        gate_bias = const.tile([P, WORD, P], F32)
+        for t in range(WORD):
+            nc.tensor.matmul(atom_h_ps[:, t, :], lhsT=wcf[:, t, :], rhs=atoms_t[:], start=True, stop=True)
+        for t in range(WORD):
+            nc.vector.tensor_scalar_add(out=gate[:, t, :], in0=atom_h_ps[:, t, :], scalar1=bcf[:, t : t + 1])
+        for t in range(SLOTS_SCALAR):
+            nc.vector.tensor_scalar_mul(out=gate_bias[:, t, :], in0=gate[:, t, :], scalar1=bdf[:, t : t + 1])
 
         total = const.tile([P, J_ROUND, P], F32)
         nc.vector.memset(total[:], 0.0)
 
+        dist_banks = {}
+        dist_grouped = {}
         dist_codes = {}
         dist_scales = {}
-        gated_h = {}
-        gated_rows = {}
-        gated_pair_banks = {}
+        dist_h = {}
+        gated_slots = {}
         gated_grouped = {}
         gated_codes = {}
         gated_scales = {}
+        pair_out = {}
+        squashed = {}
 
-        def pairs_out_of_psum(bank, grouped, b):
-            nc.scalar.copy(
-                out=grouped[:, WORD * P * J_BANK * b : WORD * P * J_BANK * (b + 1)]
-                .bitcast(F32)
-                .rearrange("p (j i u) -> p j i u", j=J_BANK, i=P, u=PAIRS),
-                in_=bank[:].rearrange("p j u i -> p j i u"),
-            )
-
-        def transpose_and_quantise_distances(r):
+        def transpose_distances(r):
             pairs = dist_rows[r][:].bitcast(F32)
-            grouped = work.tile([P, WORD * COLS], BF16, align_bytes=64, name="dist_grouped")
+            dist_banks[r] = []
             for b in range(BANKS_ROUND):
                 bank = psum.tile([P, J_BANK, PAIRS, P], F32, tag="bank", name="dist_bank")
                 for j in range(J_BANK):
                     for u in range(PAIRS):
                         nc.tensor.transpose(bank[:, j, u, :], pairs[:, J_BANK * b + j, u : ND // PAIR : PAIRS], ident_f32[:])
-                pairs_out_of_psum(bank, grouped, b)
+                dist_banks[r].append(bank)
+
+        def group_distances(r):
+            grouped = work.tile([P, WORD * COLS], BF16, align_bytes=64, name="dist_grouped")
+            for b in range(BANKS_ROUND):
+                nc.scalar.copy(
+                    out=grouped[:, WORD * P * J_BANK * b : WORD * P * J_BANK * (b + 1)]
+                    .bitcast(F32)
+                    .rearrange("p (j i u) -> p j i u", j=J_BANK, i=P, u=PAIRS),
+                    in_=dist_banks[r][b][:].rearrange("p j u i -> p j i u"),
+                )
+            dist_grouped[r] = grouped
+
+        def quantise_distances(r):
             codes = held.tile([P, COLS], U32, align_bytes=64, name="dist_codes")
             scales = held.tile([P, COLS], U8, align_bytes=64, name="dist_scales")
-            nc.vector.quantize_mx(out=codes[:].bitcast(FP8X4), scales=scales[:], in_=grouped[:])
+            nc.vector.quantize_mx(out=codes[:].bitcast(FP8X4), scales=scales[:], in_=dist_grouped[r][:])
             dist_codes[r] = codes
             dist_scales[r] = scales
 
-        def first_matmul_and_gate(r):
-            gated = held.tile([P, CHUNKS, COLS], BF16, name="gated_h")
-            for c in range(CHUNKS):
+        def first_matmul(r):
+            dist_h[r] = []
+            for t in range(WORD):
                 acc = psum.tile([P, COLS], F32, tag="bank", name="dist_h")
                 nc.tensor.matmul_mx(
                     out=acc[:],
-                    lhsT=wdf_words[:, P * c : P * (c + 1)].bitcast(FP8X4),
-                    lhsT_scale=wdf_scales[:, P * c : P * (c + 1)],
+                    lhsT=wdf_words[:, P * t : P * (t + 1)].bitcast(FP8X4),
+                    lhsT_scale=wdf_scales[:, P * t : P * (t + 1)],
                     rhs=dist_codes[r][:].bitcast(FP8X4),
                     rhs_scale=dist_scales[r][:],
                     start=True,
                     stop=True,
                 )
+                dist_h[r].append(acc)
+
+        def apply_gate(r):
+            gated = held.tile([P, WORD, COLS], BF16, name="gated_slots")
+            for t in range(SLOTS_SCALAR):
+                for s in range(J_ROUND):
+                    j = J_ROUND * r + s
+                    nc.scalar.activation(
+                        out=gated[:, t, P * s : P * (s + 1)],
+                        in_=dist_h[r][t][:, P * s : P * (s + 1)],
+                        func=ACT.Identity,
+                        scale=gate[:, t, j : j + 1],
+                        bias=gate_bias[:, t, j : j + 1],
+                    )
+            for t in range(SLOTS_SCALAR, WORD):
                 nc.vector.scalar_tensor_tensor(
-                    out=gated[:, c, :].rearrange("m (j i) -> m j i", j=J_ROUND),
-                    in0=acc[:].rearrange("m (j i) -> m j i", j=J_ROUND),
-                    scalar=bias_cols[:, CHUNKS + c : CHUNKS + c + 1],
-                    in1=atom_h_t[:, c, J_ROUND * r : J_ROUND * (r + 1)].unsqueeze(2).to_broadcast([P, J_ROUND, P]),
+                    out=gated[:, t, :].rearrange("m (j i) -> m j i", j=J_ROUND),
+                    in0=dist_h[r][t][:].rearrange("m (j i) -> m j i", j=J_ROUND),
+                    scalar=bdf[:, t : t + 1],
+                    in1=gate[:, t, J_ROUND * r : J_ROUND * (r + 1)].unsqueeze(2).to_broadcast([P, J_ROUND, P]),
                     op0=ADD,
                     op1=MULT,
                 )
-            gated_h[r] = gated
-
-        def gated_to_rows(r):
-            rows = held.tile([P, J_ROUND, PAIRS, NH // PAIRS], BF16, name="gated_rows")
-            chunk_cols = CHUNK_WORDS * PAIR
-            for b in range(BANKS_ROUND):
-                bank = psum.tile([P, J_BANK, PAIRS, NH // PAIRS], BF16, tag="bank", name="rows_bank")
-                for j in range(J_BANK):
-                    for c in range(CHUNKS):
-                        first = P * (J_BANK * b + j)
-                        nc.tensor.transpose(
-                            bank[:, j, :, chunk_cols * c : chunk_cols * (c + 1)],
-                            gated_h[r][:, c, first : first + P],
-                            sort_pairs[:],
-                        )
-                nc.scalar.copy(out=rows[:, J_BANK * b : J_BANK * (b + 1), :, :], in_=bank[:])
-            gated_rows[r] = rows
-
-        def gated_to_pairs(r):
-            pairs = gated_rows[r][:].rearrange("i j u w -> i j (u w)").bitcast(F32)
-            banks = []
-            for b in range(BANKS_ROUND):
-                bank = psum.tile([P, J_BANK, PAIRS, P], F32, tag="bank", name="words_bank")
-                for j in range(J_BANK):
-                    for u in range(PAIRS):
-                        nc.tensor.transpose(bank[:, j, u, :], pairs[:, J_BANK * b + j, P * u : P * (u + 1)], ident_f32[:])
-                banks.append(bank)
-            gated_pair_banks[r] = banks
+            gated_slots[r] = gated
 
         def group_gated(r):
-            grouped = work.tile([P, WORD * COLS], BF16, align_bytes=64, name="gated_grouped")
-            for b in range(BANKS_ROUND):
-                pairs_out_of_psum(gated_pair_banks[r][b], grouped, b)
+            grouped = work.tile([P, COLS, WORD], BF16, align_bytes=64, name="gated_grouped")
+            nc.vector.tensor_copy(out=grouped[:], in_=gated_slots[r][:].rearrange("p t c -> p c t"))
             gated_grouped[r] = grouped
 
         def quantise_gated(r):
             codes = held.tile([P, COLS], U32, align_bytes=64, name="gated_codes")
             scales = held.tile([P, COLS], U8, align_bytes=64, name="gated_scales")
-            nc.vector.quantize_mx(out=codes[:].bitcast(FP8X4), scales=scales[:], in_=gated_grouped[r][:])
+            nc.vector.quantize_mx(
+                out=codes[:].bitcast(FP8X4), scales=scales[:], in_=gated_grouped[r][:].rearrange("p c t -> p (c t)")
+            )
             gated_codes[r] = codes
             gated_scales[r] = scales
 
-        def second_matmul_and_sum(r):
+        def second_matmul(r):
             acc = psum_o.tile([P, J_ROUND, P], F32, name="pair_out")
             for s in range(J_ROUND):
                 nc.tensor.matmul_mx(
@@ -241,34 +256,46 @@ def tile_dtnnstep_pa_t_kernel(
                     start=True,
                     stop=True,
                 )
-            squashed = work.tile([P, J_ROUND, P], F32, name="squashed")
+            pair_out[r] = acc
+
+        def squash(r):
+            result = held.tile([P, J_ROUND, P], F32, name="squashed")
             for s in range(J_ROUND):
                 nc.scalar.activation(
-                    out=squashed[:, s, :],
-                    in_=acc[:, s, :],
-                    func=mybir.ActivationFunctionType.Tanh,
+                    out=result[:, s, :],
+                    in_=pair_out[r][:, s, :],
+                    func=ACT.Tanh,
                     scale=pair_weight[:, J_ROUND * r + s : J_ROUND * r + s + 1],
                 )
-            nc.vector.tensor_tensor(out=total[:], in0=total[:], in1=squashed[:], op=ADD)
+            squashed[r] = result
+
+        def add_up(r):
+            nc.vector.tensor_tensor(out=total[:], in0=total[:], in1=squashed[r][:], op=ADD)
 
         def live(r):
             return 0 <= r < ROUNDS
 
-        for step in range(ROUNDS + LAG_SECOND_MATMUL):
+        for step in range(ROUNDS + LAG_SUM + 1):
+            if live(step - LAG_SUM):
+                add_up(step - LAG_SUM)
             if live(step - LAG_QUANTISE_GATED):
                 group_gated(step - LAG_QUANTISE_GATED)
+            if live(step - LAG_QUANTISE_DISTANCES):
+                group_distances(step - LAG_QUANTISE_DISTANCES)
             if live(step - LAG_FIRST_MATMUL):
-                first_matmul_and_gate(step - LAG_FIRST_MATMUL)
+                first_matmul(step - LAG_FIRST_MATMUL)
+            if live(step - LAG_QUANTISE_DISTANCES):
+                quantise_distances(step - LAG_QUANTISE_DISTANCES)
+            if live(step - LAG_SECOND_MATMUL):
+                second_matmul(step - LAG_SECOND_MATMUL)
+            if live(step - LAG_FIRST_MATMUL):
+                apply_gate(step - LAG_FIRST_MATMUL)
             if live(step - LAG_QUANTISE_GATED):
                 quantise_gated(step - LAG_QUANTISE_GATED)
             if live(step - LAG_SECOND_MATMUL):
-                second_matmul_and_sum(step - LAG_SECOND_MATMUL)
+                squash(step - LAG_SECOND_MATMUL)
             if live(step):
-                transpose_and_quantise_distances(step)
-            if live(step - LAG_TO_ROWS):
-                gated_to_rows(step - LAG_TO_ROWS)
-            if live(step - LAG_TO_WORDS):
-                gated_to_pairs(step - LAG_TO_WORDS)
+                transpose_distances(step)
 
         summed = const.tile([P, P], F32)
         nc.vector.tensor_reduce(

@@ -27,7 +27,7 @@ COLS = J_ROUND * P
 J_BANK = 2
 BANKS_ROUND = J_ROUND // J_BANK
 
-SLOTS_SCALAR = 3
+SLOTS_SCALAR = 2
 
 FLOPS = 2 * P * P * ND * NH + 2 * P * P * NH * P + 2 * P * P * NH
 
@@ -56,8 +56,8 @@ def tile_dtnnstep_pa_t_kernel(
     with tc.tile_pool(name="const", bufs=1) as const, tc.tile_pool(name="dist", bufs=1) as dist, tc.tile_pool(
         name="work", bufs=2
     ) as work, tc.tile_pool(name="held", bufs=3) as held, tc.psum_pool(name="psum_o", bufs=1) as psum_o, tc.psum_pool(
-        name="psum", bufs=7
-    ) as psum, tc.manual_schedule():
+        name="psum_sum", bufs=1
+    ) as psum_sum, tc.psum_pool(name="psum", bufs=6) as psum, tc.manual_schedule():
         dist_rows = {}
 
         def load_distance_rows(r):
@@ -149,8 +149,7 @@ def tile_dtnnstep_pa_t_kernel(
         for t in range(SLOTS_SCALAR):
             nc.vector.tensor_scalar_mul(out=gate_bias[:, t, :], in0=gate[:, t, :], scalar1=bdf[:, t : t + 1])
 
-        total = const.tile([P, J_ROUND, P], F32)
-        nc.vector.memset(total[:], 0.0)
+        total_t = psum_sum.tile([P, P], F32)
 
         dist_banks = {}
         dist_grouped = {}
@@ -270,14 +269,21 @@ def tile_dtnnstep_pa_t_kernel(
             squashed[r] = result
 
         def add_up(r):
-            nc.vector.tensor_tensor(out=total[:], in0=total[:], in1=squashed[r][:], op=ADD)
+            for s in range(J_ROUND):
+                j = J_ROUND * r + s
+                nc.tensor.matmul(
+                    total_t[:],
+                    lhsT=squashed[r][:, s, :],
+                    rhs=ident_f32[:],
+                    is_transpose=True,
+                    start=(j == 0),
+                    stop=(j == P - 1),
+                )
 
         def live(r):
             return 0 <= r < ROUNDS
 
         for step in range(ROUNDS + LAG_SUM + 1):
-            if live(step - LAG_SUM):
-                add_up(step - LAG_SUM)
             if live(step - LAG_QUANTISE_GATED):
                 group_gated(step - LAG_QUANTISE_GATED)
             if live(step - LAG_QUANTISE_DISTANCES):
@@ -294,13 +300,15 @@ def tile_dtnnstep_pa_t_kernel(
                 quantise_gated(step - LAG_QUANTISE_GATED)
             if live(step - LAG_SECOND_MATMUL):
                 squash(step - LAG_SECOND_MATMUL)
+            if live(step - LAG_SUM):
+                add_up(step - LAG_SUM)
             if live(step):
                 transpose_distances(step)
 
-        summed = const.tile([P, P], F32)
-        nc.vector.tensor_reduce(
-            out=summed[:], in_=total[:].rearrange("i s n -> i n s"), axis=mybir.AxisListType.X, op=ADD
-        )
+        summed_t = const.tile([P, P], F32)
+        nc.vector.tensor_copy(out=summed_t[:], in_=total_t[:])
+        summed = psum.tile([P, P], F32, tag="bank")
+        nc.tensor.transpose(summed[:], summed_t[:], ident_f32[:])
         result = const.tile([P, P], F32)
         nc.vector.tensor_tensor(out=result[:], in0=summed[:], in1=atoms[:], op=ADD)
         nc.sync.dma_start(out=out[0], in_=result[:])

@@ -27,7 +27,7 @@ COLS = J_ROUND * P
 J_BANK = 2
 BANKS_ROUND = J_ROUND // J_BANK
 
-SLOTS_SCALAR = 2
+SLOTS_SCALAR = 3
 
 FLOPS = 2 * P * P * ND * NH + 2 * P * P * NH * P + 2 * P * P * NH
 

@@ -27,7 +27,7 @@ COLS = J_ROUND * P
 J_BANK = 2
 BANKS_ROUND = J_ROUND // J_BANK
 
-SLOTS_SCALAR = 3
+J_SCALAR = (2, 4, 4, 0)
 
 FLOPS = 2 * P * P * ND * NH + 2 * P * P * NH * P + 2 * P * P * NH
 
@@ -146,7 +146,7 @@ def tile_dtnnstep_pa_t_kernel(
             nc.tensor.matmul(atom_h_ps[:, t, :], lhsT=wcf[:, t, :], rhs=atoms_t[:], start=True, stop=True)
         for t in range(WORD):
             nc.vector.tensor_scalar_add(out=gate[:, t, :], in0=atom_h_ps[:, t, :], scalar1=bcf[:, t : t + 1])
-        for t in range(SLOTS_SCALAR):
+        for t in range(WORD):
             nc.vector.tensor_scalar_mul(out=gate_bias[:, t, :], in0=gate[:, t, :], scalar1=bdf[:, t : t + 1])
 
         total_t = psum_sum.tile([P, P], F32)
@@ -208,8 +208,8 @@ def tile_dtnnstep_pa_t_kernel(
 
         def apply_gate(r):
             gated = held.tile([P, WORD, COLS], BF16, name="gated_slots")
-            for t in range(SLOTS_SCALAR):
-                for s in range(J_ROUND):
+            for t in range(WORD):
+                for s in range(J_SCALAR[t]):
                     j = J_ROUND * r + s
                     nc.scalar.activation(
                         out=gated[:, t, P * s : P * (s + 1)],
@@ -218,15 +218,19 @@ def tile_dtnnstep_pa_t_kernel(
                         scale=gate[:, t, j : j + 1],
                         bias=gate_bias[:, t, j : j + 1],
                     )
-            for t in range(SLOTS_SCALAR, WORD):
-                nc.vector.scalar_tensor_tensor(
-                    out=gated[:, t, :].rearrange("m (j i) -> m j i", j=J_ROUND),
-                    in0=dist_h[r][t][:].rearrange("m (j i) -> m j i", j=J_ROUND),
-                    scalar=bdf[:, t : t + 1],
-                    in1=gate[:, t, J_ROUND * r : J_ROUND * (r + 1)].unsqueeze(2).to_broadcast([P, J_ROUND, P]),
-                    op0=ADD,
-                    op1=MULT,
-                )
+            for t in range(WORD):
+                first = J_SCALAR[t]
+                if first < J_ROUND:
+                    nc.vector.scalar_tensor_tensor(
+                        out=gated[:, t, P * first :].rearrange("m (j i) -> m j i", i=P),
+                        in0=dist_h[r][t][:, P * first :].rearrange("m (j i) -> m j i", i=P),
+                        scalar=bdf[:, t : t + 1],
+                        in1=gate[:, t, J_ROUND * r + first : J_ROUND * (r + 1)]
+                        .unsqueeze(2)
+                        .to_broadcast([P, J_ROUND - first, P]),
+                        op0=ADD,
+                        op1=MULT,
+                    )
             gated_slots[r] = gated
 
         def group_gated(r):

@@ -235,7 +235,10 @@ def tile_dtnnstep_pa_t_kernel(
 
         def group_gated(r):
             grouped = work.tile([P, COLS, WORD], BF16, align_bytes=64, name="gated_grouped")
-            nc.vector.tensor_copy(out=grouped[:], in_=gated_slots[r][:].rearrange("p t c -> p c t"))
+            nc.vector.tensor_copy(
+                out=grouped[:].rearrange("p (c i) t -> p c t i", i=WORD),
+                in_=gated_slots[r][:].rearrange("p t (c i) -> p c t i", i=WORD),
+            )
             gated_grouped[r] = grouped
 
         def quantise_gated(r):

@@ -65,8 +65,7 @@ def tile_dtnnstep_pa_t_kernel(
             nc.sync.dma_start(out=rows[:], in_=distance_matrix[0, :, J_ROUND * r : J_ROUND * (r + 1), :])
             dist_rows[r] = rows
 
-        for r in range(LAG_FIRST_MATMUL):
-            load_distance_rows(r)
+        load_distance_rows(0)
 
         wdf_scales_loaded = const.tile([P, NH], U8, align_bytes=64)
         wfc_scales = const.tile([P, P], U8, align_bytes=64)
@@ -83,6 +82,7 @@ def tile_dtnnstep_pa_t_kernel(
                 out=wdf_scales_loaded[QUADRANT * quad : QUADRANT * quad + SCALE_ROWS, :].bitcast(I32),
                 in_=W_df_scales[0, SCALE_ROWS * quad : SCALE_ROWS * (quad + 1), :].bitcast(I32),
             )
+        load_distance_rows(1)
         nc.sync.dma_start(out=wfc_words[:].bitcast(I32), in_=W_fc_words[0].rearrange("p n t -> p (n t)").bitcast(I32))
         for quad in range(QUADRANTS):
             nc.sync.dma_start(
@@ -106,13 +106,32 @@ def tile_dtnnstep_pa_t_kernel(
         nc.vector.memset(warm_in[:], 0.0)
         nc.scalar.activation(out=warm_out[:], in_=warm_in[:], func=ACT.Tanh)
 
-        for r in range(LAG_FIRST_MATMUL, ROUNDS):
+        for r in range(2, ROUNDS):
             load_distance_rows(r)
 
         ident_bf = const.tile([P, P], BF16)
         ident_f32 = const.tile([P, P], F32)
-        make_identity(nc, ident_f32[:])
         make_identity(nc, ident_bf[:])
+        make_identity(nc, ident_f32[:])
+
+        bcf = const.tile([P, WORD], F32)
+        bdf = const.tile([P, WORD], F32)
+        nc.vector.tensor_copy(out=bcf[:], in_=bcf_bf[:])
+        nc.vector.tensor_copy(out=bdf[:], in_=bdf_bf[:])
+
+        atoms_t_ps = psum.tile([P, P], BF16, tag="bank")
+        nc.tensor.transpose(atoms_t_ps[:], atoms[:], ident_bf[:])
+        atoms_t = const.tile([P, P], BF16)
+        nc.vector.tensor_copy(out=atoms_t[:], in_=atoms_t_ps[:])
+        wcf = const.tile([P, WORD, P], BF16)
+        nc.vector.tensor_copy(out=wcf[:], in_=wcf_loaded[:].rearrange("f (m t) -> f t m", t=WORD))
+
+        atom_h_ps = psum.tile([P, WORD, P], F32, tag="bank")
+        gate = const.tile([P, WORD, P], F32)
+        for t in range(WORD):
+            nc.tensor.matmul(atom_h_ps[:, t, :], lhsT=wcf[:, t, :], rhs=atoms_t[:], start=True, stop=True)
+        for t in range(WORD):
+            nc.vector.tensor_scalar_add(out=gate[:, t, :], in0=atom_h_ps[:, t, :], scalar1=bcf[:, t : t + 1])
 
         wdf_words = const.tile([P, NH], U32, align_bytes=64)
         wdf_scales = const.tile([P, NH], U8, align_bytes=64)
@@ -124,30 +143,15 @@ def tile_dtnnstep_pa_t_kernel(
             out=wdf_scales[:].rearrange("p (t m) -> p m t", t=WORD),
             in_=wdf_scales_loaded[:].rearrange("p (m t) -> p m t", t=WORD),
         )
-        wcf = const.tile([P, WORD, P], BF16)
-        nc.vector.tensor_copy(out=wcf[:], in_=wcf_loaded[:].rearrange("f (m t) -> f t m", t=WORD))
 
-        pair_weight = const.tile([P, P], F32)
-        nc.vector.tensor_copy(out=pair_weight[:], in_=pair_weight_bf[:])
-        bcf = const.tile([P, WORD], F32)
-        bdf = const.tile([P, WORD], F32)
-        nc.vector.tensor_copy(out=bcf[:], in_=bcf_bf[:])
-        nc.vector.tensor_copy(out=bdf[:], in_=bdf_bf[:])
-
-        atoms_t_ps = psum.tile([P, P], BF16, tag="bank")
-        nc.tensor.transpose(atoms_t_ps[:], atoms[:], ident_bf[:])
-        atoms_t = const.tile([P, P], BF16)
-        nc.vector.tensor_copy(out=atoms_t[:], in_=atoms_t_ps[:])
-
-        atom_h_ps = psum.tile([P, WORD, P], F32, tag="bank")
-        gate = const.tile([P, WORD, P], F32)
         gate_bias = const.tile([P, WORD, P], F32)
-        for t in range(WORD):
-            nc.tensor.matmul(atom_h_ps[:, t, :], lhsT=wcf[:, t, :], rhs=atoms_t[:], start=True, stop=True)
-        for t in range(WORD):
-            nc.vector.tensor_scalar_add(out=gate[:, t, :], in0=atom_h_ps[:, t, :], scalar1=bcf[:, t : t + 1])
-        for t in range(WORD):
-            nc.vector.tensor_scalar_mul(out=gate_bias[:, t, :], in0=gate[:, t, :], scalar1=bdf[:, t : t + 1])
+        pair_weight = const.tile([P, P], F32)
+
+        def late_constants():
+            for t in range(WORD):
+                if J_SCALAR[t] > 0:
+                    nc.vector.tensor_scalar_mul(out=gate_bias[:, t, :], in0=gate[:, t, :], scalar1=bdf[:, t : t + 1])
+            nc.vector.tensor_copy(out=pair_weight[:], in_=pair_weight_bf[:])
 
         total_t = psum_sum.tile([P, P], F32)
 
@@ -233,20 +237,29 @@ def tile_dtnnstep_pa_t_kernel(
                     )
             gated_slots[r] = gated
 
+        def parts(r):
+            if r < ROUNDS - 1:
+                return [slice(0, COLS)]
+            return [slice(0, COLS // 2), slice(COLS // 2, COLS)]
+
         def group_gated(r):
             grouped = work.tile([P, COLS, WORD], BF16, align_bytes=64, name="gated_grouped")
-            nc.vector.tensor_copy(
-                out=grouped[:].rearrange("p (c i) t -> p c t i", i=WORD),
-                in_=gated_slots[r][:].rearrange("p t (c i) -> p c t i", i=WORD),
-            )
+            for cols in parts(r):
+                nc.vector.tensor_copy(
+                    out=grouped[:, cols, :].rearrange("p (c i) t -> p c t i", i=WORD),
+                    in_=gated_slots[r][:, :, cols].rearrange("p t (c i) -> p c t i", i=WORD),
+                )
             gated_grouped[r] = grouped
 
         def quantise_gated(r):
             codes = held.tile([P, COLS], U32, align_bytes=64, name="gated_codes")
             scales = held.tile([P, COLS], U8, align_bytes=64, name="gated_scales")
-            nc.vector.quantize_mx(
-                out=codes[:].bitcast(FP8X4), scales=scales[:], in_=gated_grouped[r][:].rearrange("p c t -> p (c t)")
-            )
+            for cols in parts(r):
+                nc.vector.quantize_mx(
+                    out=codes[:, cols].bitcast(FP8X4),
+                    scales=scales[:, cols],
+                    in_=gated_grouped[r][:, cols, :].rearrange("p c t -> p (c t)"),
+                )
             gated_codes[r] = codes
             gated_scales[r] = scales
 
@@ -284,13 +297,13 @@ def tile_dtnnstep_pa_t_kernel(
                     rhs=ident_f32[:],
                     is_transpose=True,
                     start=(j == 0),
-                    stop=(j == P - 1),
+                    stop=(j == J_ROUND * (ROUNDS - 1) - 1),
                 )
 
         def live(r):
             return 0 <= r < ROUNDS
 
-        for step in range(ROUNDS + LAG_SUM + 1):
+        for step in range(ROUNDS + LAG_SECOND_MATMUL - 1):
             if live(step - LAG_QUANTISE_GATED):
                 group_gated(step - LAG_QUANTISE_GATED)
             if live(step - LAG_QUANTISE_DISTANCES):
@@ -299,6 +312,8 @@ def tile_dtnnstep_pa_t_kernel(
                 first_matmul(step - LAG_FIRST_MATMUL)
             if live(step - LAG_QUANTISE_DISTANCES):
                 quantise_distances(step - LAG_QUANTISE_DISTANCES)
+            if step == LAG_QUANTISE_DISTANCES:
+                late_constants()
             if live(step - LAG_SECOND_MATMUL):
                 second_matmul(step - LAG_SECOND_MATMUL)
             if live(step - LAG_FIRST_MATMUL):
@@ -312,10 +327,22 @@ def tile_dtnnstep_pa_t_kernel(
             if live(step):
                 transpose_distances(step)
 
+        last = ROUNDS - 1
+        add_up(last - 1)
         summed_t = const.tile([P, P], F32)
         nc.vector.tensor_copy(out=summed_t[:], in_=total_t[:])
+        second_matmul(last)
         summed = psum.tile([P, P], F32, tag="bank")
         nc.tensor.transpose(summed[:], summed_t[:], ident_f32[:])
+        squash(last)
+        first_half = const.tile([P, P], F32)
+        second_half = const.tile([P, P], F32)
+        with_residual = const.tile([P, P], F32)
+        all_but_half = const.tile([P, P], F32)
         result = const.tile([P, P], F32)
-        nc.vector.tensor_tensor(out=result[:], in0=summed[:], in1=atoms[:], op=ADD)
+        nc.vector.tensor_tensor(out=with_residual[:], in0=summed[:], in1=atoms[:], op=ADD)
+        nc.vector.tensor_tensor(out=first_half[:], in0=squashed[last][:, 0, :], in1=squashed[last][:, 1, :], op=ADD)
+        nc.vector.tensor_tensor(out=all_but_half[:], in0=with_residual[:], in1=first_half[:], op=ADD)
+        nc.vector.tensor_tensor(out=second_half[:], in0=squashed[last][:, 2, :], in1=squashed[last][:, 3, :], op=ADD)
+        nc.vector.tensor_tensor(out=result[:], in0=all_but_half[:], in1=second_half[:], op=ADD)
         nc.sync.dma_start(out=out[0], in_=result[:])

@@ -28,6 +28,7 @@ J_BANK = 2
 BANKS_ROUND = J_ROUND // J_BANK
 
 J_SCALAR = (2, 4, 4, 0)
+RELIEF_EVERY = 3
 
 FLOPS = 2 * P * P * ND * NH + 2 * P * P * NH * P + 2 * P * P * NH
 
@@ -210,10 +211,15 @@ def tile_dtnnstep_pa_t_kernel(
                 )
                 dist_h[r].append(acc)
 
+        def scalar_share(r, t):
+            if t == 0 and r % RELIEF_EVERY == RELIEF_EVERY - 1:
+                return J_SCALAR[t] - 1
+            return J_SCALAR[t]
+
         def apply_gate(r):
             gated = held.tile([P, WORD, COLS], BF16, name="gated_slots")
             for t in range(WORD):
-                for s in range(J_SCALAR[t]):
+                for s in range(scalar_share(r, t)):
                     j = J_ROUND * r + s
                     nc.scalar.activation(
                         out=gated[:, t, P * s : P * (s + 1)],
@@ -223,7 +229,7 @@ def tile_dtnnstep_pa_t_kernel(
                         bias=gate_bias[:, t, j : j + 1],
                     )
             for t in range(WORD):
-                first = J_SCALAR[t]
+                first = scalar_share(r, t)
                 if first < J_ROUND:
                     nc.vector.scalar_tensor_tensor(
                         out=gated[:, t, P * first :].rearrange("m (j i) -> m j i", i=P),

@@ -22,10 +22,11 @@ QUADRANT = P // QUADRANTS
 SCALE_ROWS = 4
 
 J_ROUND = 4
-ROUNDS = P // J_ROUND
-COLS = J_ROUND * P
+J_SHORT = J_ROUND // 2
+J_COUNT = [J_SHORT, J_SHORT] + [J_ROUND] * (P // J_ROUND - 1)
+ROUNDS = len(J_COUNT)
+J_FIRST = [sum(J_COUNT[:r]) for r in range(ROUNDS)]
 J_BANK = 2
-BANKS_ROUND = J_ROUND // J_BANK
 
 J_SCALAR = (2, 4, 4, 0)
 RELIEF_EVERY = 3
@@ -62,11 +63,10 @@ def tile_dtnnstep_pa_t_kernel(
         dist_rows = {}
 
         def load_distance_rows(r):
-            rows = dist.tile([P, J_ROUND, ND], BF16, name="dist_rows%d" % r)
-            nc.sync.dma_start(out=rows[:], in_=distance_matrix[0, :, J_ROUND * r : J_ROUND * (r + 1), :])
+            rows = dist.tile([P, J_COUNT[r], ND], BF16, name="dist_rows%d" % r)
+            nc.sync.dma_start(out=rows[:], in_=distance_matrix[0, :, J_FIRST[r] : J_FIRST[r] + J_COUNT[r], :])
             dist_rows[r] = rows
 
-        load_distance_rows(0)
 
         wdf_scales_loaded = const.tile([P, NH], U8, align_bytes=64)
         wfc_scales = const.tile([P, P], U8, align_bytes=64)
@@ -75,14 +75,15 @@ def tile_dtnnstep_pa_t_kernel(
 
         wdf_words_loaded = const.tile([P, NH], U32, align_bytes=64)
         wfc_words = const.tile([P, P], U32, align_bytes=64)
-        nc.sync.dma_start(
-            out=wdf_words_loaded[:].bitcast(I32), in_=W_df_words[0].rearrange("p n t -> p (n t)").bitcast(I32)
-        )
+        load_distance_rows(0)
         for quad in range(QUADRANTS):
             nc.sync.dma_start(
                 out=wdf_scales_loaded[QUADRANT * quad : QUADRANT * quad + SCALE_ROWS, :].bitcast(I32),
                 in_=W_df_scales[0, SCALE_ROWS * quad : SCALE_ROWS * (quad + 1), :].bitcast(I32),
             )
+        nc.sync.dma_start(
+            out=wdf_words_loaded[:].bitcast(I32), in_=W_df_words[0].rearrange("p n t -> p (n t)").bitcast(I32)
+        )
         load_distance_rows(1)
         nc.sync.dma_start(out=wfc_words[:].bitcast(I32), in_=W_fc_words[0].rearrange("p n t -> p (n t)").bitcast(I32))
         for quad in range(QUADRANTS):
@@ -115,24 +116,22 @@ def tile_dtnnstep_pa_t_kernel(
         make_identity(nc, ident_bf[:])
         make_identity(nc, ident_f32[:])
 
-        bcf = const.tile([P, WORD], F32)
         bdf = const.tile([P, WORD], F32)
-        nc.vector.tensor_copy(out=bcf[:], in_=bcf_bf[:])
-        nc.vector.tensor_copy(out=bdf[:], in_=bdf_bf[:])
+        pair_weight = const.tile([P, P], F32)
+        nc.gpsimd.tensor_copy(out=bdf[:], in_=bdf_bf[:])
+        nc.gpsimd.tensor_copy(out=pair_weight[:], in_=pair_weight_bf[:])
 
         atoms_t_ps = psum.tile([P, P], BF16, tag="bank")
         nc.tensor.transpose(atoms_t_ps[:], atoms[:], ident_bf[:])
         atoms_t = const.tile([P, P], BF16)
         nc.vector.tensor_copy(out=atoms_t[:], in_=atoms_t_ps[:])
-        wcf = const.tile([P, WORD, P], BF16)
-        nc.vector.tensor_copy(out=wcf[:], in_=wcf_loaded[:].rearrange("f (m t) -> f t m", t=WORD))
-
         atom_h_ps = psum.tile([P, WORD, P], F32, tag="bank")
         gate = const.tile([P, WORD, P], F32)
         for t in range(WORD):
-            nc.tensor.matmul(atom_h_ps[:, t, :], lhsT=wcf[:, t, :], rhs=atoms_t[:], start=True, stop=True)
-        for t in range(WORD):
-            nc.vector.tensor_scalar_add(out=gate[:, t, :], in0=atom_h_ps[:, t, :], scalar1=bcf[:, t : t + 1])
+            nc.tensor.matmul(atom_h_ps[:, t, :], lhsT=wcf_loaded[:, t:NH:WORD], rhs=atoms_t[:], start=True, stop=True)
+        nc.vector.tensor_tensor(
+            out=gate[:], in0=atom_h_ps[:], in1=bcf_bf[:].unsqueeze(2).to_broadcast([P, WORD, P]), op=ADD
+        )
 
         wdf_words = const.tile([P, NH], U32, align_bytes=64)
         wdf_scales = const.tile([P, NH], U8, align_bytes=64)
@@ -146,13 +145,13 @@ def tile_dtnnstep_pa_t_kernel(
         )
 
         gate_bias = const.tile([P, WORD, P], F32)
-        pair_weight = const.tile([P, P], F32)
 
         def late_constants():
             for t in range(WORD):
                 if J_SCALAR[t] > 0:
-                    nc.vector.tensor_scalar_mul(out=gate_bias[:, t, :], in0=gate[:, t, :], scalar1=bdf[:, t : t + 1])
-            nc.vector.tensor_copy(out=pair_weight[:], in_=pair_weight_bf[:])
+                    nc.scalar.activation(
+                        out=gate_bias[:, t, :], in_=gate[:, t, :], func=ACT.Copy, scale=bdf[:, t : t + 1]
+                    )
 
         total_t = psum_sum.tile([P, P], F32)
 
@@ -171,7 +170,7 @@ def tile_dtnnstep_pa_t_kernel(
         def transpose_distances(r):
             pairs = dist_rows[r][:].bitcast(F32)
             dist_banks[r] = []
-            for b in range(BANKS_ROUND):
+            for b in range(J_COUNT[r] // J_BANK):
                 bank = psum.tile([P, J_BANK, PAIRS, P], F32, tag="bank", name="dist_bank")
                 for j in range(J_BANK):
                     for u in range(PAIRS):
@@ -179,8 +178,8 @@ def tile_dtnnstep_pa_t_kernel(
                 dist_banks[r].append(bank)
 
         def group_distances(r):
-            grouped = work.tile([P, WORD * COLS], BF16, align_bytes=64, name="dist_grouped")
-            for b in range(BANKS_ROUND):
+            grouped = work.tile([P, WORD * P * J_COUNT[r]], BF16, align_bytes=64, name="dist_grouped")
+            for b in range(J_COUNT[r] // J_BANK):
                 nc.scalar.copy(
                     out=grouped[:, WORD * P * J_BANK * b : WORD * P * J_BANK * (b + 1)]
                     .bitcast(F32)
@@ -190,8 +189,8 @@ def tile_dtnnstep_pa_t_kernel(
             dist_grouped[r] = grouped
 
         def quantise_distances(r):
-            codes = held.tile([P, COLS], U32, align_bytes=64, name="dist_codes")
-            scales = held.tile([P, COLS], U8, align_bytes=64, name="dist_scales")
+            codes = held.tile([P, P * J_COUNT[r]], U32, align_bytes=64, name="dist_codes")
+            scales = held.tile([P, P * J_COUNT[r]], U8, align_bytes=64, name="dist_scales")
             nc.vector.quantize_mx(out=codes[:].bitcast(FP8X4), scales=scales[:], in_=dist_grouped[r][:])
             dist_codes[r] = codes
             dist_scales[r] = scales
@@ -199,7 +198,7 @@ def tile_dtnnstep_pa_t_kernel(
         def first_matmul(r):
             dist_h[r] = []
             for t in range(WORD):
-                acc = psum.tile([P, COLS], F32, tag="bank", name="dist_h")
+                acc = psum.tile([P, P * J_COUNT[r]], F32, tag="bank", name="dist_h")
                 nc.tensor.matmul_mx(
                     out=acc[:],
                     lhsT=wdf_words[:, P * t : P * (t + 1)].bitcast(FP8X4),
@@ -212,15 +211,16 @@ def tile_dtnnstep_pa_t_kernel(
                 dist_h[r].append(acc)
 
         def scalar_share(r, t):
-            if t == 0 and r % RELIEF_EVERY == RELIEF_EVERY - 1:
-                return J_SCALAR[t] - 1
-            return J_SCALAR[t]
+            share = J_SCALAR[t]
+            if t == 0:
+                share = [4, 0, 0][r % 3] if r < ROUNDS - 3 else 4
+            return share * J_COUNT[r] // J_ROUND
 
         def apply_gate(r):
-            gated = held.tile([P, WORD, COLS], BF16, name="gated_slots")
+            gated = held.tile([P, WORD, P * J_COUNT[r]], BF16, name="gated_slots")
             for t in range(WORD):
                 for s in range(scalar_share(r, t)):
-                    j = J_ROUND * r + s
+                    j = J_FIRST[r] + s
                     nc.scalar.activation(
                         out=gated[:, t, P * s : P * (s + 1)],
                         in_=dist_h[r][t][:, P * s : P * (s + 1)],
@@ -230,26 +230,27 @@ def tile_dtnnstep_pa_t_kernel(
                     )
             for t in range(WORD):
                 first = scalar_share(r, t)
-                if first < J_ROUND:
+                if first < J_COUNT[r]:
                     nc.vector.scalar_tensor_tensor(
                         out=gated[:, t, P * first :].rearrange("m (j i) -> m j i", i=P),
                         in0=dist_h[r][t][:, P * first :].rearrange("m (j i) -> m j i", i=P),
                         scalar=bdf[:, t : t + 1],
-                        in1=gate[:, t, J_ROUND * r + first : J_ROUND * (r + 1)]
+                        in1=gate[:, t, J_FIRST[r] + first : J_FIRST[r] + J_COUNT[r]]
                         .unsqueeze(2)
-                        .to_broadcast([P, J_ROUND - first, P]),
+                        .to_broadcast([P, J_COUNT[r] - first, P]),
                         op0=ADD,
                         op1=MULT,
                     )
             gated_slots[r] = gated
 
         def parts(r):
+            cols = P * J_COUNT[r]
             if r < ROUNDS - 1:
-                return [slice(0, COLS)]
-            return [slice(0, COLS // 2), slice(COLS // 2, COLS)]
+                return [slice(0, cols)]
+            return [slice(0, cols // 2), slice(cols // 2, cols)]
 
         def group_gated(r):
-            grouped = work.tile([P, COLS, WORD], BF16, align_bytes=64, name="gated_grouped")
+            grouped = work.tile([P, P * J_COUNT[r], WORD], BF16, align_bytes=64, name="gated_grouped")
             for cols in parts(r):
                 nc.vector.tensor_copy(
                     out=grouped[:, cols, :].rearrange("p (c i) t -> p c t i", i=WORD),
@@ -258,8 +259,8 @@ def tile_dtnnstep_pa_t_kernel(
             gated_grouped[r] = grouped
 
         def quantise_gated(r):
-            codes = held.tile([P, COLS], U32, align_bytes=64, name="gated_codes")
-            scales = held.tile([P, COLS], U8, align_bytes=64, name="gated_scales")
+            codes = held.tile([P, P * J_COUNT[r]], U32, align_bytes=64, name="gated_codes")
+            scales = held.tile([P, P * J_COUNT[r]], U8, align_bytes=64, name="gated_scales")
             for cols in parts(r):
                 nc.vector.quantize_mx(
                     out=codes[:, cols].bitcast(FP8X4),
@@ -270,8 +271,8 @@ def tile_dtnnstep_pa_t_kernel(
             gated_scales[r] = scales
 
         def second_matmul(r):
-            acc = psum_o.tile([P, J_ROUND, P], F32, name="pair_out")
-            for s in range(J_ROUND):
+            acc = psum_o.tile([P, J_COUNT[r], P], F32, name="pair_out")
+            for s in range(J_COUNT[r]):
                 nc.tensor.matmul_mx(
                     out=acc[:, s, :],
                     lhsT=gated_codes[r][:, P * s : P * (s + 1)].bitcast(FP8X4),
@@ -284,26 +285,26 @@ def tile_dtnnstep_pa_t_kernel(
             pair_out[r] = acc
 
         def squash(r):
-            result = held.tile([P, J_ROUND, P], F32, name="squashed")
-            for s in range(J_ROUND):
+            result = held.tile([P, J_COUNT[r], P], F32, name="squashed")
+            for s in range(J_COUNT[r]):
                 nc.scalar.activation(
                     out=result[:, s, :],
                     in_=pair_out[r][:, s, :],
                     func=ACT.Tanh,
-                    scale=pair_weight[:, J_ROUND * r + s : J_ROUND * r + s + 1],
+                    scale=pair_weight[:, J_FIRST[r] + s : J_FIRST[r] + s + 1],
                 )
             squashed[r] = result
 
         def add_up(r):
-            for s in range(J_ROUND):
-                j = J_ROUND * r + s
+            for s in range(J_COUNT[r]):
+                j = J_FIRST[r] + s
                 nc.tensor.matmul(
                     total_t[:],
                     lhsT=squashed[r][:, s, :],
                     rhs=ident_f32[:],
                     is_transpose=True,
                     start=(j == 0),
-                    stop=(j == J_ROUND * (ROUNDS - 1) - 1),
+                    stop=(j == J_FIRST[ROUNDS - 1] - 1),
                 )
 
         def live(r):
@@ -314,12 +315,12 @@ def tile_dtnnstep_pa_t_kernel(
                 group_gated(step - LAG_QUANTISE_GATED)
             if live(step - LAG_QUANTISE_DISTANCES):
                 group_distances(step - LAG_QUANTISE_DISTANCES)
+            if step == LAG_QUANTISE_DISTANCES:
+                late_constants()
             if live(step - LAG_FIRST_MATMUL):
                 first_matmul(step - LAG_FIRST_MATMUL)
             if live(step - LAG_QUANTISE_DISTANCES):
                 quantise_distances(step - LAG_QUANTISE_DISTANCES)
-            if step == LAG_QUANTISE_DISTANCES:
-                late_constants()
             if live(step - LAG_SECOND_MATMUL):
                 second_matmul(step - LAG_SECOND_MATMUL)
             if live(step - LAG_FIRST_MATMUL):
@@ -348,7 +349,7 @@ def tile_dtnnstep_pa_t_kernel(
         result = const.tile([P, P], F32)
         nc.vector.tensor_tensor(out=with_residual[:], in0=summed[:], in1=atoms[:], op=ADD)
         nc.vector.tensor_tensor(out=first_half[:], in0=squashed[last][:, 0, :], in1=squashed[last][:, 1, :], op=ADD)
-        nc.vector.tensor_tensor(out=all_but_half[:], in0=with_residual[:], in1=first_half[:], op=ADD)
         nc.vector.tensor_tensor(out=second_half[:], in0=squashed[last][:, 2, :], in1=squashed[last][:, 3, :], op=ADD)
+        nc.vector.tensor_tensor(out=all_but_half[:], in0=with_residual[:], in1=first_half[:], op=ADD)
         nc.vector.tensor_tensor(out=result[:], in0=all_but_half[:], in1=second_half[:], op=ADD)
         nc.sync.dma_start(out=out[0], in_=result[:])

@@ -75,78 +75,60 @@ def tile_dtnnstep_pa_t_kernel(
 
         wdf_words_loaded = const.tile([P, NH], U32, align_bytes=64)
         wfc_words = const.tile([P, P], U32, align_bytes=64)
-        load_distance_rows(0)
-        for quad in range(QUADRANTS):
-            nc.sync.dma_start(
-                out=wdf_scales_loaded[QUADRANT * quad : QUADRANT * quad + SCALE_ROWS, :].bitcast(I32),
-                in_=W_df_scales[0, SCALE_ROWS * quad : SCALE_ROWS * (quad + 1), :].bitcast(I32),
-            )
-        nc.sync.dma_start(
-            out=wdf_words_loaded[:].bitcast(I32), in_=W_df_words[0].rearrange("p n t -> p (n t)").bitcast(I32)
-        )
-        load_distance_rows(1)
-        nc.sync.dma_start(out=wfc_words[:].bitcast(I32), in_=W_fc_words[0].rearrange("p n t -> p (n t)").bitcast(I32))
-        for quad in range(QUADRANTS):
-            nc.sync.dma_start(
-                out=wfc_scales[QUADRANT * quad : QUADRANT * quad + SCALE_ROWS, :].bitcast(I32),
-                in_=W_fc_scales[0, SCALE_ROWS * quad : SCALE_ROWS * (quad + 1), :].bitcast(I32),
-            )
+
+        def load_words(tile, words):
+            nc.sync.dma_start(out=tile[:].bitcast(I32), in_=words[0].rearrange("p n t -> p (n t)").bitcast(I32))
+
+        def load_scales(tile, scales):
+            for quad in range(QUADRANTS):
+                nc.sync.dma_start(
+                    out=tile[QUADRANT * quad : QUADRANT * quad + SCALE_ROWS, :].bitcast(I32),
+                    in_=scales[0, SCALE_ROWS * quad : SCALE_ROWS * (quad + 1), :].bitcast(I32),
+                )
 
         atoms = const.tile([P, P], BF16)
         wcf_loaded = const.tile([P, NH], BF16)
         pair_weight_bf = const.tile([P, P], BF16)
         bcf_bf = const.tile([P, WORD], BF16)
         bdf_bf = const.tile([P, WORD], BF16)
+
+        load_distance_rows(0)
         nc.scalar.dma_start(out=atoms[:], in_=atom_features[0])
-        nc.scalar.dma_start(out=wcf_loaded[:], in_=W_cf)
-        nc.scalar.dma_start(out=bcf_bf[:], in_=b_cf.rearrange("(p t) -> p t", t=WORD))
-        nc.scalar.dma_start(out=bdf_bf[:], in_=b_df.rearrange("(p t) -> p t", t=WORD))
-        nc.scalar.dma_start(out=pair_weight_bf[:], in_=distance_matrix_mask[0])
+        load_words(wdf_words_loaded, W_df_words)
+        load_scales(wdf_scales_loaded, W_df_scales)
+        load_distance_rows(1)
+        ident_bf = const.tile([P, P], BF16)
+        ident_f32 = const.tile([P, P], F32)
+        nc.gpsimd.dma_start(out=wcf_loaded[:], in_=W_cf)
+        make_identity(nc, ident_f32[:])
+        nc.gpsimd.dma_start(out=bcf_bf[:], in_=b_cf.rearrange("(p t) -> p t", t=WORD))
+        make_identity(nc, ident_bf[:])
+        nc.gpsimd.dma_start(out=bdf_bf[:], in_=b_df.rearrange("(p t) -> p t", t=WORD))
+        nc.gpsimd.dma_start(out=pair_weight_bf[:], in_=distance_matrix_mask[0])
 
         warm_in = const.tile([P, 1], F32)
         warm_out = const.tile([P, 1], F32)
         nc.vector.memset(warm_in[:], 0.0)
         nc.scalar.activation(out=warm_out[:], in_=warm_in[:], func=ACT.Tanh)
 
-        for r in range(2, ROUNDS):
+        load_distance_rows(2)
+        load_words(wfc_words, W_fc_words)
+        load_scales(wfc_scales, W_fc_scales)
+        for r in range(3, ROUNDS):
             load_distance_rows(r)
 
-        ident_bf = const.tile([P, P], BF16)
-        ident_f32 = const.tile([P, P], F32)
-        make_identity(nc, ident_bf[:])
-        make_identity(nc, ident_f32[:])
 
         bdf = const.tile([P, WORD], F32)
         pair_weight = const.tile([P, P], F32)
         nc.gpsimd.tensor_copy(out=bdf[:], in_=bdf_bf[:])
         nc.gpsimd.tensor_copy(out=pair_weight[:], in_=pair_weight_bf[:])
 
-        atoms_t_ps = psum.tile([P, P], BF16, tag="bank")
-        nc.tensor.transpose(atoms_t_ps[:], atoms[:], ident_bf[:])
-        atoms_t = const.tile([P, P], BF16)
-        nc.vector.tensor_copy(out=atoms_t[:], in_=atoms_t_ps[:])
-        atom_h_ps = psum.tile([P, WORD, P], F32, tag="bank")
-        gate = const.tile([P, WORD, P], F32)
-        for t in range(WORD):
-            nc.tensor.matmul(atom_h_ps[:, t, :], lhsT=wcf_loaded[:, t:NH:WORD], rhs=atoms_t[:], start=True, stop=True)
-        nc.vector.tensor_tensor(
-            out=gate[:], in0=atom_h_ps[:], in1=bcf_bf[:].unsqueeze(2).to_broadcast([P, WORD, P]), op=ADD
-        )
-
-        wdf_words = const.tile([P, NH], U32, align_bytes=64)
-        wdf_scales = const.tile([P, NH], U8, align_bytes=64)
-        nc.vector.tensor_copy(
-            out=wdf_words[:].bitcast(I32).rearrange("p (t m) -> p t m", t=WORD),
-            in_=wdf_words_loaded[:].bitcast(I32).rearrange("p (m t) -> p t m", t=WORD),
-        )
-        nc.vector.tensor_copy(
-            out=wdf_scales[:].rearrange("p (t m) -> p m t", t=WORD),
-            in_=wdf_scales_loaded[:].rearrange("p (m t) -> p m t", t=WORD),
-        )
-
         gate_bias = const.tile([P, WORD, P], F32)
 
         def late_constants():
+            nc.vector.tensor_tensor(
+                out=gate[:], in0=atom_h_ps[:], in1=bcf_bf[:].unsqueeze(2).to_broadcast([P, WORD, P]), op=ADD
+            )
             for t in range(WORD):
                 if J_SCALAR[t] > 0:
                     nc.scalar.activation(
@@ -213,7 +195,7 @@ def tile_dtnnstep_pa_t_kernel(
         def scalar_share(r, t):
             share = J_SCALAR[t]
             if t == 0:
-                share = [4, 0, 0][r % 3] if r < ROUNDS - 3 else 4
+                share = 4 if r == ROUNDS - 1 else [2, 2, 1][r % 3]
             return share * J_COUNT[r] // J_ROUND
 
         def apply_gate(r):
@@ -310,17 +292,39 @@ def tile_dtnnstep_pa_t_kernel(
         def live(r):
             return 0 <= r < ROUNDS
 
+        transpose_distances(0)
+
+        atoms_t_ps = psum.tile([P, P], BF16, tag="bank")
+        nc.tensor.transpose(atoms_t_ps[:], atoms[:], ident_bf[:])
+        atoms_t = const.tile([P, P], BF16)
+        nc.vector.tensor_copy(out=atoms_t[:], in_=atoms_t_ps[:])
+        atom_h_ps = psum.tile([P, WORD, P], F32, tag="bank")
+        gate = const.tile([P, WORD, P], F32)
+        for t in range(WORD):
+            nc.tensor.matmul(atom_h_ps[:, t, :], lhsT=wcf_loaded[:, t:NH:WORD], rhs=atoms_t[:], start=True, stop=True)
+
+        wdf_words = const.tile([P, NH], U32, align_bytes=64)
+        wdf_scales = const.tile([P, NH], U8, align_bytes=64)
+        nc.vector.tensor_copy(
+            out=wdf_words[:].bitcast(I32).rearrange("p (t m) -> p t m", t=WORD),
+            in_=wdf_words_loaded[:].bitcast(I32).rearrange("p (m t) -> p t m", t=WORD),
+        )
+        nc.vector.tensor_copy(
+            out=wdf_scales[:].rearrange("p (t m) -> p m t", t=WORD),
+            in_=wdf_scales_loaded[:].rearrange("p (m t) -> p m t", t=WORD),
+        )
+
         for step in range(ROUNDS + LAG_SECOND_MATMUL - 1):
             if live(step - LAG_QUANTISE_GATED):
                 group_gated(step - LAG_QUANTISE_GATED)
             if live(step - LAG_QUANTISE_DISTANCES):
                 group_distances(step - LAG_QUANTISE_DISTANCES)
-            if step == LAG_QUANTISE_DISTANCES:
-                late_constants()
             if live(step - LAG_FIRST_MATMUL):
                 first_matmul(step - LAG_FIRST_MATMUL)
             if live(step - LAG_QUANTISE_DISTANCES):
                 quantise_distances(step - LAG_QUANTISE_DISTANCES)
+            if step == LAG_QUANTISE_DISTANCES:
+                late_constants()
             if live(step - LAG_SECOND_MATMUL):
                 second_matmul(step - LAG_SECOND_MATMUL)
             if live(step - LAG_FIRST_MATMUL):
@@ -331,7 +335,7 @@ def tile_dtnnstep_pa_t_kernel(
                 squash(step - LAG_SECOND_MATMUL)
             if live(step - LAG_SUM):
                 add_up(step - LAG_SUM)
-            if live(step):
+            if live(step) and step > 0:
                 transpose_distances(step)
 
         last = ROUNDS - 1

@@ -23,7 +23,7 @@ SCALE_ROWS = 4
 
 J_ROUND = 4
 J_SHORT = J_ROUND // 2
-J_COUNT = [J_SHORT, J_SHORT] + [J_ROUND] * (P // J_ROUND - 1)
+J_COUNT = [J_ROUND] * (P // J_ROUND)
 ROUNDS = len(J_COUNT)
 J_FIRST = [sum(J_COUNT[:r]) for r in range(ROUNDS)]
 J_BANK = 2
@@ -94,29 +94,30 @@ def tile_dtnnstep_pa_t_kernel(
 
         load_distance_rows(0)
         nc.scalar.dma_start(out=atoms[:], in_=atom_features[0])
+        nc.scalar.dma_start(out=wcf_loaded[:], in_=W_cf)
         load_words(wdf_words_loaded, W_df_words)
         load_scales(wdf_scales_loaded, W_df_scales)
         load_distance_rows(1)
-        ident_bf = const.tile([P, P], BF16)
-        ident_f32 = const.tile([P, P], F32)
-        nc.gpsimd.dma_start(out=wcf_loaded[:], in_=W_cf)
-        make_identity(nc, ident_f32[:])
-        nc.gpsimd.dma_start(out=bcf_bf[:], in_=b_cf.rearrange("(p t) -> p t", t=WORD))
-        make_identity(nc, ident_bf[:])
-        nc.gpsimd.dma_start(out=bdf_bf[:], in_=b_df.rearrange("(p t) -> p t", t=WORD))
-        nc.gpsimd.dma_start(out=pair_weight_bf[:], in_=distance_matrix_mask[0])
 
         warm_in = const.tile([P, 1], F32)
         warm_out = const.tile([P, 1], F32)
         nc.vector.memset(warm_in[:], 0.0)
         nc.scalar.activation(out=warm_out[:], in_=warm_in[:], func=ACT.Tanh)
 
+        nc.scalar.dma_start(out=bcf_bf[:], in_=b_cf.rearrange("(p t) -> p t", t=WORD))
+        nc.scalar.dma_start(out=bdf_bf[:], in_=b_df.rearrange("(p t) -> p t", t=WORD))
         load_distance_rows(2)
+        nc.scalar.dma_start(out=pair_weight_bf[:], in_=distance_matrix_mask[0])
         load_words(wfc_words, W_fc_words)
         load_scales(wfc_scales, W_fc_scales)
         for r in range(3, ROUNDS):
             load_distance_rows(r)
 
+
+        ident_bf = const.tile([P, P], BF16)
+        ident_f32 = const.tile([P, P], F32)
+        make_identity(nc, ident_f32[:])
+        make_identity(nc, ident_bf[:])
 
         bdf = const.tile([P, WORD], F32)
         pair_weight = const.tile([P, P], F32)
@@ -194,9 +195,9 @@ def tile_dtnnstep_pa_t_kernel(
 
         def scalar_share(r, t):
             share = J_SCALAR[t]
-            if t == 0:
-                share = 4 if r == ROUNDS - 1 else [2, 2, 1][r % 3]
-            return share * J_COUNT[r] // J_ROUND
+            if t == 0 and r % RELIEF_EVERY == RELIEF_EVERY - 1:
+                share = share - 1
+            return share
 
         def apply_gate(r):
             gated = held.tile([P, WORD, P * J_COUNT[r]], BF16, name="gated_slots")

@@ -30,6 +30,7 @@ J_BANK = 2
 
 J_SCALAR = (2, 4, 4, 0)
 RELIEF_EVERY = 3
+LAST_SCALAR = (4, 4, 4, 0)
 
 FLOPS = 2 * P * P * ND * NH + 2 * P * P * NH * P + 2 * P * P * NH
 
@@ -131,7 +132,7 @@ def tile_dtnnstep_pa_t_kernel(
                 out=gate[:], in0=atom_h_ps[:], in1=bcf_bf[:].unsqueeze(2).to_broadcast([P, WORD, P]), op=ADD
             )
             for t in range(WORD):
-                if J_SCALAR[t] > 0:
+                if max(J_SCALAR[t], LAST_SCALAR[t]) > 0:
                     nc.scalar.activation(
                         out=gate_bias[:, t, :], in_=gate[:, t, :], func=ACT.Copy, scale=bdf[:, t : t + 1]
                     )
@@ -195,22 +196,26 @@ def tile_dtnnstep_pa_t_kernel(
 
         def scalar_share(r, t):
             share = J_SCALAR[t]
+            if r == ROUNDS - 1:
+                return LAST_SCALAR[t]
             if t == 0 and r % RELIEF_EVERY == RELIEF_EVERY - 1:
                 share = share - 1
             return share
 
         def apply_gate(r):
             gated = held.tile([P, WORD, P * J_COUNT[r]], BF16, name="gated_slots")
-            for t in range(WORD):
-                for s in range(scalar_share(r, t)):
-                    j = J_FIRST[r] + s
-                    nc.scalar.activation(
-                        out=gated[:, t, P * s : P * (s + 1)],
-                        in_=dist_h[r][t][:, P * s : P * (s + 1)],
-                        func=ACT.Identity,
-                        scale=gate[:, t, j : j + 1],
-                        bias=gate_bias[:, t, j : j + 1],
-                    )
+            pieces = [(t, s) for t in range(WORD) for s in range(scalar_share(r, t))]
+            if r == ROUNDS - 1:
+                pieces = sorted(pieces, key=lambda piece: piece[1] // J_BANK)
+            for t, s in pieces:
+                j = J_FIRST[r] + s
+                nc.scalar.activation(
+                    out=gated[:, t, P * s : P * (s + 1)],
+                    in_=dist_h[r][t][:, P * s : P * (s + 1)],
+                    func=ACT.Identity,
+                    scale=gate[:, t, j : j + 1],
+                    bias=gate_bias[:, t, j : j + 1],
+                )
             for t in range(WORD):
                 first = scalar_share(r, t)
                 if first < J_COUNT[r]:

import concourse.mybir as mybir
from concourse.masks import make_identity

F32 = mybir.dt.float32
BF16 = mybir.dt.bfloat16
I32 = mybir.dt.int32
U32 = mybir.dt.uint32
U8 = mybir.dt.uint8
FP8X4 = mybir.dt.float8_e4m3fn_x4
ADD = mybir.AluOpType.add
MULT = mybir.AluOpType.mult
ACT = mybir.ActivationFunctionType

P = 128
ND = 512
NH = 512
WORD = 4
PAIRS = 2
PAIR = 2
QUADRANTS = 4
QUADRANT = P // QUADRANTS
SCALE_ROWS = 4

J_ROUND = 4
J_SHORT = J_ROUND // 2
J_COUNT = [J_ROUND] * (P // J_ROUND)
ROUNDS = len(J_COUNT)
J_FIRST = [sum(J_COUNT[:r]) for r in range(ROUNDS)]
J_BANK = 2

J_SCALAR = (2, 4, 4, 0)
RELIEF_EVERY = 3
LAST_SCALAR = (4, 4, 4, 0)

FLOPS = 2 * P * P * ND * NH + 2 * P * P * NH * P + 2 * P * P * NH

LAG_QUANTISE_DISTANCES = 1
LAG_FIRST_MATMUL = 2
LAG_QUANTISE_GATED = 3
LAG_SECOND_MATMUL = 4
LAG_SUM = 5


def tile_dtnnstep_pa_t_kernel(
    tc,
    atom_features,
    distance_matrix,
    distance_matrix_mask,
    W_cf,
    W_df_words,
    W_df_scales,
    W_fc_words,
    W_fc_scales,
    b_cf,
    b_df,
    out,
):
    nc = tc.nc
    with tc.tile_pool(name="const", bufs=1) as const, tc.tile_pool(name="dist", bufs=1) as dist, tc.tile_pool(
        name="work", bufs=2
    ) as work, tc.tile_pool(name="held", bufs=3) as held, tc.psum_pool(name="psum_o", bufs=1) as psum_o, tc.psum_pool(
        name="psum_sum", bufs=1
    ) as psum_sum, tc.psum_pool(name="psum", bufs=6) as psum, tc.manual_schedule():
        dist_rows = {}

        def load_distance_rows(r):
            rows = dist.tile([P, J_COUNT[r], ND], BF16, name="dist_rows%d" % r)
            nc.sync.dma_start(out=rows[:], in_=distance_matrix[0, :, J_FIRST[r] : J_FIRST[r] + J_COUNT[r], :])
            dist_rows[r] = rows


        wdf_scales_loaded = const.tile([P, NH], U8, align_bytes=64)
        wfc_scales = const.tile([P, P], U8, align_bytes=64)
        nc.vector.memset(wdf_scales_loaded[:].bitcast(I32), 0)
        nc.vector.memset(wfc_scales[:].bitcast(I32), 0)

        wdf_words_loaded = const.tile([P, NH], U32, align_bytes=64)
        wfc_words = const.tile([P, P], U32, align_bytes=64)

        def load_words(tile, words):
            nc.sync.dma_start(out=tile[:].bitcast(I32), in_=words[0].rearrange("p n t -> p (n t)").bitcast(I32))

        def load_scales(tile, scales):
            for quad in range(QUADRANTS):
                nc.sync.dma_start(
                    out=tile[QUADRANT * quad : QUADRANT * quad + SCALE_ROWS, :].bitcast(I32),
                    in_=scales[0, SCALE_ROWS * quad : SCALE_ROWS * (quad + 1), :].bitcast(I32),
                )

        atoms = const.tile([P, P], BF16)
        wcf_loaded = const.tile([P, NH], BF16)
        pair_weight_bf = const.tile([P, P], BF16)
        bcf_bf = const.tile([P, WORD], BF16)
        bdf_bf = const.tile([P, WORD], BF16)

        load_distance_rows(0)
        nc.scalar.dma_start(out=atoms[:], in_=atom_features[0])
        nc.scalar.dma_start(out=wcf_loaded[:], in_=W_cf)
        load_words(wdf_words_loaded, W_df_words)
        load_scales(wdf_scales_loaded, W_df_scales)
        load_distance_rows(1)

        warm_in = const.tile([P, 1], F32)
        warm_out = const.tile([P, 1], F32)
        nc.vector.memset(warm_in[:], 0.0)
        nc.scalar.activation(out=warm_out[:], in_=warm_in[:], func=ACT.Tanh)

        nc.scalar.dma_start(out=bcf_bf[:], in_=b_cf.rearrange("(p t) -> p t", t=WORD))
        nc.scalar.dma_start(out=bdf_bf[:], in_=b_df.rearrange("(p t) -> p t", t=WORD))
        load_distance_rows(2)
        nc.scalar.dma_start(out=pair_weight_bf[:], in_=distance_matrix_mask[0])
        load_words(wfc_words, W_fc_words)
        load_scales(wfc_scales, W_fc_scales)
        for r in range(3, ROUNDS):
            load_distance_rows(r)


        ident_bf = const.tile([P, P], BF16)
        ident_f32 = const.tile([P, P], F32)
        make_identity(nc, ident_f32[:])
        make_identity(nc, ident_bf[:])

        bdf = const.tile([P, WORD], F32)
        pair_weight = const.tile([P, P], F32)
        nc.gpsimd.tensor_copy(out=bdf[:], in_=bdf_bf[:])
        nc.gpsimd.tensor_copy(out=pair_weight[:], in_=pair_weight_bf[:])

        gate_bias = const.tile([P, WORD, P], F32)

        def late_constants():
            nc.vector.tensor_tensor(
                out=gate[:], in0=atom_h_ps[:], in1=bcf_bf[:].unsqueeze(2).to_broadcast([P, WORD, P]), op=ADD
            )
            for t in range(WORD):
                if max(J_SCALAR[t], LAST_SCALAR[t]) > 0:
                    nc.scalar.activation(
                        out=gate_bias[:, t, :], in_=gate[:, t, :], func=ACT.Copy, scale=bdf[:, t : t + 1]
                    )

        total_t = psum_sum.tile([P, P], F32)

        dist_banks = {}
        dist_grouped = {}
        dist_codes = {}
        dist_scales = {}
        dist_h = {}
        gated_slots = {}
        gated_grouped = {}
        gated_codes = {}
        gated_scales = {}
        pair_out = {}
        squashed = {}

        def transpose_distances(r):
            pairs = dist_rows[r][:].bitcast(F32)
            dist_banks[r] = []
            for b in range(J_COUNT[r] // J_BANK):
                bank = psum.tile([P, J_BANK, PAIRS, P], F32, tag="bank", name="dist_bank")
                for j in range(J_BANK):
                    for u in range(PAIRS):
                        nc.tensor.transpose(bank[:, j, u, :], pairs[:, J_BANK * b + j, u : ND // PAIR : PAIRS], ident_f32[:])
                dist_banks[r].append(bank)

        def group_distances(r):
            grouped = work.tile([P, WORD * P * J_COUNT[r]], BF16, align_bytes=64, name="dist_grouped")
            for b in range(J_COUNT[r] // J_BANK):
                nc.scalar.copy(
                    out=grouped[:, WORD * P * J_BANK * b : WORD * P * J_BANK * (b + 1)]
                    .bitcast(F32)
                    .rearrange("p (j i u) -> p j i u", j=J_BANK, i=P, u=PAIRS),
                    in_=dist_banks[r][b][:].rearrange("p j u i -> p j i u"),
                )
            dist_grouped[r] = grouped

        def quantise_distances(r):
            codes = held.tile([P, P * J_COUNT[r]], U32, align_bytes=64, name="dist_codes")
            scales = held.tile([P, P * J_COUNT[r]], U8, align_bytes=64, name="dist_scales")
            nc.vector.quantize_mx(out=codes[:].bitcast(FP8X4), scales=scales[:], in_=dist_grouped[r][:])
            dist_codes[r] = codes
            dist_scales[r] = scales

        def first_matmul(r):
            dist_h[r] = []
            for t in range(WORD):
                acc = psum.tile([P, P * J_COUNT[r]], F32, tag="bank", name="dist_h")
                nc.tensor.matmul_mx(
                    out=acc[:],
                    lhsT=wdf_words[:, P * t : P * (t + 1)].bitcast(FP8X4),
                    lhsT_scale=wdf_scales[:, P * t : P * (t + 1)],
                    rhs=dist_codes[r][:].bitcast(FP8X4),
                    rhs_scale=dist_scales[r][:],
                    start=True,
                    stop=True,
                )
                dist_h[r].append(acc)

        def scalar_share(r, t):
            share = J_SCALAR[t]
            if r == ROUNDS - 1:
                return LAST_SCALAR[t]
            if t == 0 and r % RELIEF_EVERY == RELIEF_EVERY - 1:
                share = share - 1
            return share

        def apply_gate(r):
            gated = held.tile([P, WORD, P * J_COUNT[r]], BF16, name="gated_slots")
            pieces = [(t, s) for t in range(WORD) for s in range(scalar_share(r, t))]
            if r == ROUNDS - 1:
                pieces = sorted(pieces, key=lambda piece: piece[1] // J_BANK)
            for t, s in pieces:
                j = J_FIRST[r] + s
                nc.scalar.activation(
                    out=gated[:, t, P * s : P * (s + 1)],
                    in_=dist_h[r][t][:, P * s : P * (s + 1)],
                    func=ACT.Identity,
                    scale=gate[:, t, j : j + 1],
                    bias=gate_bias[:, t, j : j + 1],
                )
            for t in range(WORD):
                first = scalar_share(r, t)
                if first < J_COUNT[r]:
                    nc.vector.scalar_tensor_tensor(
                        out=gated[:, t, P * first :].rearrange("m (j i) -> m j i", i=P),
                        in0=dist_h[r][t][:, P * first :].rearrange("m (j i) -> m j i", i=P),
                        scalar=bdf[:, t : t + 1],
                        in1=gate[:, t, J_FIRST[r] + first : J_FIRST[r] + J_COUNT[r]]
                        .unsqueeze(2)
                        .to_broadcast([P, J_COUNT[r] - first, P]),
                        op0=ADD,
                        op1=MULT,
                    )
            gated_slots[r] = gated

        def parts(r):
            cols = P * J_COUNT[r]
            if r < ROUNDS - 1:
                return [slice(0, cols)]
            return [slice(0, cols // 2), slice(cols // 2, cols)]

        def group_gated(r):
            grouped = work.tile([P, P * J_COUNT[r], WORD], BF16, align_bytes=64, name="gated_grouped")
            for cols in parts(r):
                nc.vector.tensor_copy(
                    out=grouped[:, cols, :].rearrange("p (c i) t -> p c t i", i=WORD),
                    in_=gated_slots[r][:, :, cols].rearrange("p t (c i) -> p c t i", i=WORD),
                )
            gated_grouped[r] = grouped

        def quantise_gated(r):
            codes = held.tile([P, P * J_COUNT[r]], U32, align_bytes=64, name="gated_codes")
            scales = held.tile([P, P * J_COUNT[r]], U8, align_bytes=64, name="gated_scales")
            for cols in parts(r):
                nc.vector.quantize_mx(
                    out=codes[:, cols].bitcast(FP8X4),
                    scales=scales[:, cols],
                    in_=gated_grouped[r][:, cols, :].rearrange("p c t -> p (c t)"),
                )
            gated_codes[r] = codes
            gated_scales[r] = scales

        def second_matmul(r):
            acc = psum_o.tile([P, J_COUNT[r], P], F32, name="pair_out")
            for s in range(J_COUNT[r]):
                nc.tensor.matmul_mx(
                    out=acc[:, s, :],
                    lhsT=gated_codes[r][:, P * s : P * (s + 1)].bitcast(FP8X4),
                    lhsT_scale=gated_scales[r][:, P * s : P * (s + 1)],
                    rhs=wfc_words[:].bitcast(FP8X4),
                    rhs_scale=wfc_scales[:],
                    start=True,
                    stop=True,
                )
            pair_out[r] = acc

        def squash(r):
            result = held.tile([P, J_COUNT[r], P], F32, name="squashed")
            for s in range(J_COUNT[r]):
                nc.scalar.activation(
                    out=result[:, s, :],
                    in_=pair_out[r][:, s, :],
                    func=ACT.Tanh,
                    scale=pair_weight[:, J_FIRST[r] + s : J_FIRST[r] + s + 1],
                )
            squashed[r] = result

        def add_up(r):
            for s in range(J_COUNT[r]):
                j = J_FIRST[r] + s
                nc.tensor.matmul(
                    total_t[:],
                    lhsT=squashed[r][:, s, :],
                    rhs=ident_f32[:],
                    is_transpose=True,
                    start=(j == 0),
                    stop=(j == J_FIRST[ROUNDS - 1] - 1),
                )

        def live(r):
            return 0 <= r < ROUNDS

        transpose_distances(0)

        atoms_t_ps = psum.tile([P, P], BF16, tag="bank")
        nc.tensor.transpose(atoms_t_ps[:], atoms[:], ident_bf[:])
        atoms_t = const.tile([P, P], BF16)
        nc.vector.tensor_copy(out=atoms_t[:], in_=atoms_t_ps[:])
        atom_h_ps = psum.tile([P, WORD, P], F32, tag="bank")
        gate = const.tile([P, WORD, P], F32)
        for t in range(WORD):
            nc.tensor.matmul(atom_h_ps[:, t, :], lhsT=wcf_loaded[:, t:NH:WORD], rhs=atoms_t[:], start=True, stop=True)

        wdf_words = const.tile([P, NH], U32, align_bytes=64)
        wdf_scales = const.tile([P, NH], U8, align_bytes=64)
        nc.vector.tensor_copy(
            out=wdf_words[:].bitcast(I32).rearrange("p (t m) -> p t m", t=WORD),
            in_=wdf_words_loaded[:].bitcast(I32).rearrange("p (m t) -> p t m", t=WORD),
        )
        nc.vector.tensor_copy(
            out=wdf_scales[:].rearrange("p (t m) -> p m t", t=WORD),
            in_=wdf_scales_loaded[:].rearrange("p (m t) -> p m t", t=WORD),
        )

        for step in range(ROUNDS + LAG_SECOND_MATMUL - 1):
            if live(step - LAG_QUANTISE_GATED):
                group_gated(step - LAG_QUANTISE_GATED)
            if live(step - LAG_QUANTISE_DISTANCES):
                group_distances(step - LAG_QUANTISE_DISTANCES)
            if live(step - LAG_FIRST_MATMUL):
                first_matmul(step - LAG_FIRST_MATMUL)
            if live(step - LAG_QUANTISE_DISTANCES):
                quantise_distances(step - LAG_QUANTISE_DISTANCES)
            if step == LAG_QUANTISE_DISTANCES:
                late_constants()
            if live(step - LAG_SECOND_MATMUL):
                second_matmul(step - LAG_SECOND_MATMUL)
            if live(step - LAG_FIRST_MATMUL):
                apply_gate(step - LAG_FIRST_MATMUL)
            if live(step - LAG_QUANTISE_GATED):
                quantise_gated(step - LAG_QUANTISE_GATED)
            if live(step - LAG_SECOND_MATMUL):
                squash(step - LAG_SECOND_MATMUL)
            if live(step - LAG_SUM):
                add_up(step - LAG_SUM)
            if live(step) and step > 0:
                transpose_distances(step)

        last = ROUNDS - 1
        add_up(last - 1)
        summed_t = const.tile([P, P], F32)
        nc.vector.tensor_copy(out=summed_t[:], in_=total_t[:])
        second_matmul(last)
        summed = psum.tile([P, P], F32, tag="bank")
        nc.tensor.transpose(summed[:], summed_t[:], ident_f32[:])
        squash(last)
        first_half = const.tile([P, P], F32)
        second_half = const.tile([P, P], F32)
        with_residual = const.tile([P, P], F32)
        all_but_half = const.tile([P, P], F32)
        result = const.tile([P, P], F32)
        nc.vector.tensor_tensor(out=with_residual[:], in0=summed[:], in1=atoms[:], op=ADD)
        nc.vector.tensor_tensor(out=first_half[:], in0=squashed[last][:, 0, :], in1=squashed[last][:, 1, :], op=ADD)
        nc.vector.tensor_tensor(out=second_half[:], in0=squashed[last][:, 2, :], in1=squashed[last][:, 3, :], op=ADD)
        nc.vector.tensor_tensor(out=all_but_half[:], in0=with_residual[:], in1=first_half[:], op=ADD)
        nc.vector.tensor_tensor(out=result[:], in0=all_but_half[:], in1=second_half[:], op=ADD)
        nc.sync.dma_start(out=out[0], in_=result[:])
